import numpy as np
import ml_dtypes

BF16 = ml_dtypes.bfloat16


def bf(x):
    return np.asarray(x, np.float32).astype(BF16)


def f32(x):
    return np.asarray(x, np.float32)


def f64(x):
    return np.asarray(x).astype(np.float64)


def striped(idx):
    return np.tile(idx.reshape(-1, 16).T, (8, 1))


H, D, HALF, R, B, T, S, C, N, Q = 4, 128, 64, 512, 4, 512, 4096, 512, 2048, 2048
ROPE_BASE = 10000.0


def rope_tables():
    freq = np.float32(1.0) / f32(ROPE_BASE ** (np.arange(0, D, 2) / D))
    ang = f32(np.arange(T))[None, :] * freq[:, None]
    cos, sin = np.cos(f64(ang)), np.sin(f64(ang))
    return f32(np.concatenate([cos, cos])), f32(np.concatenate([-sin, sin]))


def swap_halves(a):
    return a.reshape(H, 2, HALF, -1)[:, ::-1].reshape(C, -1)


def setup_inputs():
    rc, rs = rope_tables()
    return {"kc": f32(np.random.standard_normal((C, S))), "q": f32(np.random.standard_normal((C, Q))), "vals": bf(2.0 * np.random.standard_normal((N, C))), "rc": rc, "rs": rs, "offs": striped(np.random.permutation(S)[:N])}


def reference(kc, q, vals, rc, rs, offs):
    idx = offs[:16].T.reshape(-1)
    kr = f64(kc)[:, idx] * np.tile(f64(rc), (H, B)) + swap_halves(f64(kc))[:, idx] * np.tile(f64(rs), (H, B))
    qr = f64(q) * np.tile(f64(rc)[:, T - 1:T], (H, 1)) + swap_halves(f64(q)) * np.tile(f64(rs)[:, T - 1:T], (H, 1))
    res = np.zeros((C, Q))
    for h in range(H):
        kh = kr[h * D:(h + 1) * D].reshape(D, B, T).transpose(1, 2, 0)
        qh = qr[h * D:(h + 1) * D].reshape(D, B, R).transpose(1, 0, 2)
        sc = (kh @ qh) / np.sqrt(D)
        e = np.exp(sc - sc.max(axis=1, keepdims=True))
        p = e / e.sum(axis=1, keepdims=True)
        vh = f64(vals)[:, h * D:(h + 1) * D].reshape(B, T, D).transpose(0, 2, 1)
        res[h * D:(h + 1) * D] = (vh @ p).transpose(1, 0, 2).reshape(D, Q)
    return res

@@ -1,0 +1,173 @@
+import math
+from contextlib import ExitStack
+
+import concourse.mybir as mybir
+from concourse.masks import make_identity
+
+F32 = mybir.dt.float32
+BF16 = mybir.dt.bfloat16
+U16 = mybir.dt.uint16
+MULT = mybir.AluOpType.mult
+ADD = mybir.AluOpType.add
+EXP = mybir.ActivationFunctionType.Exp
+AXIS_X = mybir.AxisListType.X
+
+P = 128
+H, D, HALF = 4, 128, 64
+B, T, R = 4, 512, 512
+S = 4096
+N = B * T
+TC = T // P
+RC = R // P
+SCALE = 1.0 / math.sqrt(D)
+FLOPS = 4 * H * B * T * R * D
+
+
+def tile_streamingattentionsink_b_kernel(tc, kc, q, vals, rc, rs, offs, out):
+    nc = tc.nc
+    with ExitStack() as ctx:
+        held = ctx.enter_context(tc.tile_pool(name="held", bufs=1))
+        q_pool = ctx.enter_context(tc.tile_pool(name="q_pool", bufs=4))
+        qr_pool = ctx.enter_context(tc.tile_pool(name="qr_pool", bufs=4))
+        rope_pool = ctx.enter_context(tc.tile_pool(name="rope_pool", bufs=3))
+        kr_pool = ctx.enter_context(tc.tile_pool(name="kr_pool", bufs=4))
+        small = ctx.enter_context(tc.tile_pool(name="small", bufs=4))
+        e_pool = ctx.enter_context(tc.tile_pool(name="e_pool", bufs=2 * RC))
+        p_pool = ctx.enter_context(tc.tile_pool(name="p_pool", bufs=4))
+        pT_pool = ctx.enter_context(tc.tile_pool(name="pT_pool", bufs=2))
+        o_pool = ctx.enter_context(tc.tile_pool(name="o_pool", bufs=2))
+        ps_s = ctx.enter_context(tc.psum_pool(name="ps_s", bufs=4))
+        ps_t = ctx.enter_context(tc.psum_pool(name="ps_t", bufs=2))
+        ps_o = ctx.enter_context(tc.psum_pool(name="ps_o", bufs=1))
+        ps_q = ctx.enter_context(tc.psum_pool(name="ps_q", bufs=1))
+
+        blocks = [(h, b) for h in range(H) for b in range(B)]
+
+        offsets = held.tile([P, N // 16], U16, name="offsets")
+        nc.sync.dma_start(offsets[:], offs)
+        rc_sb = held.tile([P, T], F32, name="rc_sb")
+        nc.sync.dma_start(rc_sb[:], rc)
+        rs_sb = held.tile([P, T], F32, name="rs_sb")
+        nc.sync.dma_start(rs_sb[:], rs)
+
+        own_rows = [held.tile([P, S], F32, name=f"own_rows{h}") for h in range(H)]
+        partner_rows = [held.tile([P, S], F32, name=f"partner_rows{h}") for h in range(H)]
+        vals_sb = held.tile([P, N // P, H * D], BF16, name="vals_sb")
+        vals_blocks = vals.rearrange("(n p) c -> p n c", p=P)
+        q_sb = {}
+
+        def load_own(h):
+            nc.sync.dma_start(own_rows[h][:], kc[h * D : (h + 1) * D, :])
+
+        def load_partner(h):
+            nc.sync.dma_start(partner_rows[h][0:HALF, :], kc[h * D + HALF : (h + 1) * D, :])
+            nc.sync.dma_start(partner_rows[h][HALF:D, :], kc[h * D : h * D + HALF, :])
+
+        def load_q(n):
+            h, b = blocks[n]
+            q_sb[n] = q_pool.tile([P, R], F32, name="q_sb")
+            nc.sync.dma_start(q_sb[n][:], q[h * D : (h + 1) * D, b * R : (b + 1) * R])
+
+        def load_vals(b):
+            nc.sync.dma_start(vals_sb[:, b * TC : (b + 1) * TC, :], vals_blocks[:, b * TC : (b + 1) * TC, :])
+
+        load_own(0)
+        load_q(0)
+        load_partner(0)
+        load_q(1)
+        load_vals(0)
+
+        ident_f = held.tile([P, P], F32, name="ident_f")
+        make_identity(nc, ident_f[:])
+        ident_b = held.tile([P, P], BF16, name="ident_b")
+        nc.vector.tensor_copy(ident_b[:], ident_f[:])
+
+        cos_q = rc_sb[:, T - 1 : T]
+        sin_q = rs_sb[:, T - 1 : T]
+        sin_diag = held.tile([P, P], F32, name="sin_diag")
+        nc.vector.tensor_scalar_mul(sin_diag[:], ident_f[:], sin_q)
+        rot = held.tile([P, P], F32, name="rot")
+        nc.vector.scalar_tensor_tensor(rot[:, 0:HALF], ident_f[:, 0:HALF], cos_q, sin_diag[:, HALF:D], MULT, ADD)
+        nc.vector.scalar_tensor_tensor(rot[:, HALF:D], ident_f[:, HALF:D], cos_q, sin_diag[:, 0:HALF], MULT, ADD)
+        rot_ps = ps_q.tile([P, P], F32, name="rot_ps", tag="q_ps")
+        nc.tensor.transpose(rot_ps[:], rot[:], ident_f[:])
+        rotT = held.tile([P, P], F32, name="rotT")
+        nc.vector.tensor_copy(rotT[:], rot_ps[:])
+
+        qr, kr, e, rowsum = {}, {}, {}, {}
+
+        def rope(n):
+            h, b = blocks[n]
+            q_ps = ps_q.tile([P, R], F32, name="q_ps")
+            nc.tensor.matmul(q_ps[:], lhsT=rotT[:], rhs=q_sb[n][:], start=True, stop=True)
+            qr[n] = qr_pool.tile([P, R], BF16, name="qr")
+            nc.vector.tensor_copy(qr[n][:], q_ps[:])
+            piece = offsets[:, b * (T // 16) : (b + 1) * (T // 16)]
+            own = rope_pool.tile([P, T], F32, name="own")
+            nc.vector.tensor_tensor(own[:], own_rows[h][:].indirect(piece), rc_sb[:], MULT)
+            partner = rope_pool.tile([P, T], F32, name="partner")
+            nc.vector.tensor_tensor(partner[:], partner_rows[h][:].indirect(piece), rs_sb[:], MULT)
+            kr[n] = kr_pool.tile([P, T], BF16, name="kr")
+            nc.gpsimd.tensor_tensor(kr[n][:], own[:], partner[:], ADD)
+
+        def scores_and_exp(n):
+            rowmax = small.tile([P, RC], F32, name="rowmax")
+            s_ps = []
+            for j in range(RC):
+                s_ps.append(ps_s.tile([P, T], F32, name="s_ps"))
+                nc.tensor.matmul(s_ps[j][:], lhsT=qr[n][:, j * P : (j + 1) * P], rhs=kr[n][:], start=True, stop=True)
+                nc.vector.reduce_max(rowmax[:, j : j + 1], s_ps[j][:], axis=AXIS_X)
+            shift = small.tile([P, RC], F32, name="shift")
+            nc.scalar.mul(shift[:], rowmax[:], -SCALE)
+            rowsum[n] = small.tile([P, RC], F32, name="rowsum")
+            e[n] = []
+            for j in range(RC):
+                e[n].append(e_pool.tile([P, T], F32, name="e"))
+                nc.scalar.activation(
+                    e[n][j][:], s_ps[j][:], EXP, bias=shift[:, j : j + 1], scale=SCALE, accum_out=rowsum[n][:, j : j + 1]
+                )
+
+        def weights_times_values(n):
+            h, b = blocks[n]
+            rinv = small.tile([P, RC], F32, name="rinv")
+            nc.vector.reciprocal(rinv[:], rowsum[n][:])
+            pT = pT_pool.tile([P, TC, R], BF16, name="pT")
+            for pair in range(RC // 2):
+                pT_ps = ps_t.tile([P, TC, 2 * P], BF16, name="pT_ps")
+                for jj in range(2):
+                    j = 2 * pair + jj
+                    p = p_pool.tile([P, T], BF16, name="p")
+                    nc.gpsimd.tensor_scalar(p[:], e[n][j][:], rinv[:, j : j + 1], 1.0, MULT, MULT)
+                    for c in range(TC):
+                        nc.tensor.transpose(pT_ps[:, c, jj * P : (jj + 1) * P], p[:, c * P : (c + 1) * P], ident_b[:])
+                nc.scalar.copy(pT[:, :, pair * 2 * P : (pair + 1) * 2 * P], pT_ps[:])
+            o_ps = ps_o.tile([P, R], F32, name="o_ps")
+            for c in range(TC):
+                nc.tensor.matmul(
+                    o_ps[:],
+                    lhsT=vals_sb[:, b * TC + c, h * D : (h + 1) * D],
+                    rhs=pT[:, c, :],
+                    start=(c == 0),
+                    stop=(c == TC - 1),
+                )
+            o_sb = o_pool.tile([P, R], F32, name="o_sb")
+            nc.scalar.copy(o_sb[:], o_ps[:])
+            nc.scalar.dma_start(out[h * D : (h + 1) * D, b * R : (b + 1) * R], o_sb[:])
+
+        rope(0)
+        rope(1)
+        scores_and_exp(0)
+        for n in range(len(blocks)):
+            h, b = blocks[n]
+            if n + 2 < len(blocks):
+                load_q(n + 2)
+            if n + 1 < B:
+                load_vals(n + 1)
+            if b == 0 and h + 1 < H:
+                load_own(h + 1)
+                load_partner(h + 1)
+            if n + 2 < len(blocks):
+                rope(n + 2)
+            if n + 1 < len(blocks):
+                scores_and_exp(n + 1)
+            weights_times_values(n)

@@ -10,6 +10,7 @@ U16 = mybir.dt.uint16
 MULT = mybir.AluOpType.mult
 ADD = mybir.AluOpType.add
 EXP = mybir.ActivationFunctionType.Exp
+COPY = mybir.ActivationFunctionType.Copy
 AXIS_X = mybir.AxisListType.X
 
 P = 128
@@ -27,21 +28,22 @@ def tile_streamingattentionsink_b_kernel(tc, kc, q, vals, rc, rs, offs, out):
     nc = tc.nc
     with ExitStack() as ctx:
         held = ctx.enter_context(tc.tile_pool(name="held", bufs=1))
-        q_pool = ctx.enter_context(tc.tile_pool(name="q_pool", bufs=4))
-        qr_pool = ctx.enter_context(tc.tile_pool(name="qr_pool", bufs=4))
-        rope_pool = ctx.enter_context(tc.tile_pool(name="rope_pool", bufs=3))
-        kr_pool = ctx.enter_context(tc.tile_pool(name="kr_pool", bufs=4))
+        q_pool = ctx.enter_context(tc.tile_pool(name="q_pool", bufs=3))
+        qr_pool = ctx.enter_context(tc.tile_pool(name="qr_pool", bufs=3))
+        rope_pool = ctx.enter_context(tc.tile_pool(name="rope_pool", bufs=4))
+        kr_pool = ctx.enter_context(tc.tile_pool(name="kr_pool", bufs=3))
         small = ctx.enter_context(tc.tile_pool(name="small", bufs=4))
         e_pool = ctx.enter_context(tc.tile_pool(name="e_pool", bufs=2 * RC))
-        p_pool = ctx.enter_context(tc.tile_pool(name="p_pool", bufs=4))
-        pT_pool = ctx.enter_context(tc.tile_pool(name="pT_pool", bufs=2))
+        bcast_pool = ctx.enter_context(tc.tile_pool(name="bcast_pool", bufs=2))
+        eT_pool = ctx.enter_context(tc.tile_pool(name="eT_pool", bufs=2))
         o_pool = ctx.enter_context(tc.tile_pool(name="o_pool", bufs=2))
         ps_s = ctx.enter_context(tc.psum_pool(name="ps_s", bufs=4))
         ps_t = ctx.enter_context(tc.psum_pool(name="ps_t", bufs=2))
         ps_o = ctx.enter_context(tc.psum_pool(name="ps_o", bufs=1))
-        ps_q = ctx.enter_context(tc.psum_pool(name="ps_q", bufs=1))
+        ps_r = ctx.enter_context(tc.psum_pool(name="ps_r", bufs=1))
 
         blocks = [(h, b) for h in range(H) for b in range(B)]
+        NB = len(blocks)
 
         offsets = held.tile([P, N // 16], U16, name="offsets")
         nc.sync.dma_start(offsets[:], offs)
@@ -54,120 +56,102 @@ def tile_streamingattentionsink_b_kernel(tc, kc, q, vals, rc, rs, offs, out):
         partner_rows = [held.tile([P, S], F32, name=f"partner_rows{h}") for h in range(H)]
         vals_sb = held.tile([P, N // P, H * D], BF16, name="vals_sb")
         vals_blocks = vals.rearrange("(n p) c -> p n c", p=P)
-        q_sb = {}
+        q_own, q_partner = {}, {}
 
-        def load_own(h):
+        def load_with_halves_exchanged(tile, rows):
+            nc.sync.dma_start(tile[0:HALF, :], rows[HALF:D, :])
+            nc.sync.dma_start(tile[HALF:D, :], rows[0:HALF, :])
+
+        def load_keys(h):
             nc.sync.dma_start(own_rows[h][:], kc[h * D : (h + 1) * D, :])
-
-        def load_partner(h):
-            nc.sync.dma_start(partner_rows[h][0:HALF, :], kc[h * D + HALF : (h + 1) * D, :])
-            nc.sync.dma_start(partner_rows[h][HALF:D, :], kc[h * D : h * D + HALF, :])
+            load_with_halves_exchanged(partner_rows[h], kc[h * D : (h + 1) * D, :])
 
         def load_q(n):
             h, b = blocks[n]
-            q_sb[n] = q_pool.tile([P, R], F32, name="q_sb")
-            nc.sync.dma_start(q_sb[n][:], q[h * D : (h + 1) * D, b * R : (b + 1) * R])
+            q_block = q[h * D : (h + 1) * D, b * R : (b + 1) * R]
+            q_own[n] = q_pool.tile([P, R], F32, name="q_own")
+            nc.sync.dma_start(q_own[n][:], q_block)
+            q_partner[n] = q_pool.tile([P, R], F32, name="q_partner")
+            load_with_halves_exchanged(q_partner[n], q_block)
 
         def load_vals(b):
             nc.sync.dma_start(vals_sb[:, b * TC : (b + 1) * TC, :], vals_blocks[:, b * TC : (b + 1) * TC, :])
 
-        load_own(0)
+        load_keys(0)
         load_q(0)
-        load_partner(0)
         load_q(1)
-        load_vals(0)
+        for b in range(B):
+            load_vals(b)
 
         ident_f = held.tile([P, P], F32, name="ident_f")
         make_identity(nc, ident_f[:])
         ident_b = held.tile([P, P], BF16, name="ident_b")
         nc.vector.tensor_copy(ident_b[:], ident_f[:])
+        cos_q = held.tile([P, 1], F32, name="cos_q")
+        nc.vector.tensor_scalar_mul(cos_q[:], rc_sb[:, T - 1 : T], SCALE)
+        sin_q = held.tile([P, 1], F32, name="sin_q")
+        nc.vector.tensor_scalar_mul(sin_q[:], rs_sb[:, T - 1 : T], SCALE)
 
-        cos_q = rc_sb[:, T - 1 : T]
-        sin_q = rs_sb[:, T - 1 : T]
-        sin_diag = held.tile([P, P], F32, name="sin_diag")
-        nc.vector.tensor_scalar_mul(sin_diag[:], ident_f[:], sin_q)
-        rot = held.tile([P, P], F32, name="rot")
-        nc.vector.scalar_tensor_tensor(rot[:, 0:HALF], ident_f[:, 0:HALF], cos_q, sin_diag[:, HALF:D], MULT, ADD)
-        nc.vector.scalar_tensor_tensor(rot[:, HALF:D], ident_f[:, HALF:D], cos_q, sin_diag[:, 0:HALF], MULT, ADD)
-        rot_ps = ps_q.tile([P, P], F32, name="rot_ps", tag="q_ps")
-        nc.tensor.transpose(rot_ps[:], rot[:], ident_f[:])
-        rotT = held.tile([P, P], F32, name="rotT")
-        nc.vector.tensor_copy(rotT[:], rot_ps[:])
-
-        qr, kr, e, rowsum = {}, {}, {}, {}
-
-        def rope(n):
+        for n in range(NB):
             h, b = blocks[n]
-            q_ps = ps_q.tile([P, R], F32, name="q_ps")
-            nc.tensor.matmul(q_ps[:], lhsT=rotT[:], rhs=q_sb[n][:], start=True, stop=True)
-            qr[n] = qr_pool.tile([P, R], BF16, name="qr")
-            nc.vector.tensor_copy(qr[n][:], q_ps[:])
+            out_block = out[h * D : (h + 1) * D, b * R : (b + 1) * R]
+            if n + 2 < NB:
+                load_q(n + 2)
+            if b == 0 and h + 1 < H:
+                load_keys(h + 1)
+
+            q_sin = qr_pool.tile([P, R], F32, name="q_sin")
+            nc.scalar.activation(q_sin[:], q_partner[n][:], COPY, scale=sin_q[:])
+            qr = qr_pool.tile([P, R], BF16, name="qr")
+            nc.vector.scalar_tensor_tensor(qr[:], q_own[n][:], cos_q[:], q_sin[:], MULT, ADD)
+
             piece = offsets[:, b * (T // 16) : (b + 1) * (T // 16)]
             own = rope_pool.tile([P, T], F32, name="own")
             nc.vector.tensor_tensor(own[:], own_rows[h][:].indirect(piece), rc_sb[:], MULT)
             partner = rope_pool.tile([P, T], F32, name="partner")
             nc.vector.tensor_tensor(partner[:], partner_rows[h][:].indirect(piece), rs_sb[:], MULT)
-            kr[n] = kr_pool.tile([P, T], BF16, name="kr")
-            nc.gpsimd.tensor_tensor(kr[n][:], own[:], partner[:], ADD)
+            kr = kr_pool.tile([P, T], BF16, name="kr")
+            nc.gpsimd.tensor_tensor(kr[:], own[:], partner[:], ADD)
 
-        def scores_and_exp(n):
-            rowmax = small.tile([P, RC], F32, name="rowmax")
-            s_ps = []
+            negmax = small.tile([P, RC], F32, name="negmax")
+            rowsum = small.tile([P, RC], F32, name="rowsum")
+            e = []
             for j in range(RC):
-                s_ps.append(ps_s.tile([P, T], F32, name="s_ps"))
-                nc.tensor.matmul(s_ps[j][:], lhsT=qr[n][:, j * P : (j + 1) * P], rhs=kr[n][:], start=True, stop=True)
-                nc.vector.reduce_max(rowmax[:, j : j + 1], s_ps[j][:], axis=AXIS_X)
-            shift = small.tile([P, RC], F32, name="shift")
-            nc.scalar.mul(shift[:], rowmax[:], -SCALE)
-            rowsum[n] = small.tile([P, RC], F32, name="rowsum")
-            e[n] = []
-            for j in range(RC):
-                e[n].append(e_pool.tile([P, T], F32, name="e"))
-                nc.scalar.activation(
-                    e[n][j][:], s_ps[j][:], EXP, bias=shift[:, j : j + 1], scale=SCALE, accum_out=rowsum[n][:, j : j + 1]
-                )
+                s_ps = ps_s.tile([P, T], F32, name="s_ps")
+                nc.tensor.matmul(s_ps[:], lhsT=qr[:, j * P : (j + 1) * P], rhs=kr[:], start=True, stop=True)
+                nc.vector.reduce_max(negmax[:, j : j + 1], s_ps[:], axis=AXIS_X, negate=True)
+                e.append(e_pool.tile([P, T], BF16, name="e"))
+                nc.scalar.activation(e[j][:], s_ps[:], EXP, bias=negmax[:, j : j + 1], accum_out=rowsum[:, j : j + 1])
 
-        def weights_times_values(n):
-            h, b = blocks[n]
             rinv = small.tile([P, RC], F32, name="rinv")
-            nc.vector.reciprocal(rinv[:], rowsum[n][:])
-            pT = pT_pool.tile([P, TC, R], BF16, name="pT")
+            nc.vector.reciprocal(rinv[:], rowsum[:])
+            rinvT_ps = ps_r.tile([RC, P], F32, name="rinvT_ps")
+            nc.tensor.transpose(rinvT_ps[:], rinv[:], ident_f[:])
+            rinvT = small.tile([RC, P], F32, name="rinvT")
+            nc.scalar.copy(rinvT[:], rinvT_ps[:])
+            nc.sync.dma_start(out_block[0:1, :].rearrange("o (j p) -> (o j) p", j=RC), rinvT[:])
+            rinv_bcast = bcast_pool.tile([P, R], F32, name="rinv_bcast")
+            nc.sync.dma_start(rinv_bcast[:], out_block[0, :].partition_broadcast(P))
+
+            eT = eT_pool.tile([P, TC, R], BF16, name="eT")
             for pair in range(RC // 2):
-                pT_ps = ps_t.tile([P, TC, 2 * P], BF16, name="pT_ps")
+                eT_ps = ps_t.tile([P, TC, 2 * P], BF16, name="eT_ps")
                 for jj in range(2):
-                    j = 2 * pair + jj
-                    p = p_pool.tile([P, T], BF16, name="p")
-                    nc.gpsimd.tensor_scalar(p[:], e[n][j][:], rinv[:, j : j + 1], 1.0, MULT, MULT)
                     for c in range(TC):
-                        nc.tensor.transpose(pT_ps[:, c, jj * P : (jj + 1) * P], p[:, c * P : (c + 1) * P], ident_b[:])
-                nc.scalar.copy(pT[:, :, pair * 2 * P : (pair + 1) * 2 * P], pT_ps[:])
+                        nc.tensor.transpose(
+                            eT_ps[:, c, jj * P : (jj + 1) * P], e[2 * pair + jj][:, c * P : (c + 1) * P], ident_b[:]
+                        )
+                nc.scalar.copy(eT[:, :, pair * 2 * P : (pair + 1) * 2 * P], eT_ps[:])
+
             o_ps = ps_o.tile([P, R], F32, name="o_ps")
             for c in range(TC):
                 nc.tensor.matmul(
                     o_ps[:],
                     lhsT=vals_sb[:, b * TC + c, h * D : (h + 1) * D],
-                    rhs=pT[:, c, :],
+                    rhs=eT[:, c, :],
                     start=(c == 0),
                     stop=(c == TC - 1),
                 )
             o_sb = o_pool.tile([P, R], F32, name="o_sb")
-            nc.scalar.copy(o_sb[:], o_ps[:])
-            nc.scalar.dma_start(out[h * D : (h + 1) * D, b * R : (b + 1) * R], o_sb[:])
-
-        rope(0)
-        rope(1)
-        scores_and_exp(0)
-        for n in range(len(blocks)):
-            h, b = blocks[n]
-            if n + 2 < len(blocks):
-                load_q(n + 2)
-            if n + 1 < B:
-                load_vals(n + 1)
-            if b == 0 and h + 1 < H:
-                load_own(h + 1)
-                load_partner(h + 1)
-            if n + 2 < len(blocks):
-                rope(n + 2)
-            if n + 1 < len(blocks):
-                scores_and_exp(n + 1)
-            weights_times_values(n)
+            nc.vector.tensor_tensor(o_sb[:], o_ps[:], rinv_bcast[:], MULT)
+            nc.sync.dma_start(out_block, o_sb[:])

@@ -28,6 +28,7 @@ def tile_streamingattentionsink_b_kernel(tc, kc, q, vals, rc, rs, offs, out):
     nc = tc.nc
     with ExitStack() as ctx:
         held = ctx.enter_context(tc.tile_pool(name="held", bufs=1))
+        key_pool = ctx.enter_context(tc.tile_pool(name="key_pool", bufs=2))
         q_pool = ctx.enter_context(tc.tile_pool(name="q_pool", bufs=3))
         qr_pool = ctx.enter_context(tc.tile_pool(name="qr_pool", bufs=3))
         rope_pool = ctx.enter_context(tc.tile_pool(name="rope_pool", bufs=4))
@@ -37,8 +38,8 @@ def tile_streamingattentionsink_b_kernel(tc, kc, q, vals, rc, rs, offs, out):
         bcast_pool = ctx.enter_context(tc.tile_pool(name="bcast_pool", bufs=2))
         eT_pool = ctx.enter_context(tc.tile_pool(name="eT_pool", bufs=2))
         o_pool = ctx.enter_context(tc.tile_pool(name="o_pool", bufs=2))
-        ps_s = ctx.enter_context(tc.psum_pool(name="ps_s", bufs=4))
-        ps_t = ctx.enter_context(tc.psum_pool(name="ps_t", bufs=2))
+        ps_s = ctx.enter_context(tc.psum_pool(name="ps_s", bufs=3))
+        ps_t = ctx.enter_context(tc.psum_pool(name="ps_t", bufs=3))
         ps_o = ctx.enter_context(tc.psum_pool(name="ps_o", bufs=1))
         ps_r = ctx.enter_context(tc.psum_pool(name="ps_r", bufs=1))
 
@@ -52,19 +53,20 @@ def tile_streamingattentionsink_b_kernel(tc, kc, q, vals, rc, rs, offs, out):
         rs_sb = held.tile([P, T], F32, name="rs_sb")
         nc.sync.dma_start(rs_sb[:], rs)
 
-        own_rows = [held.tile([P, S], F32, name=f"own_rows{h}") for h in range(H)]
-        partner_rows = [held.tile([P, S], F32, name=f"partner_rows{h}") for h in range(H)]
+        own_rows, partner_rows = {}, {}
         vals_sb = held.tile([P, N // P, H * D], BF16, name="vals_sb")
         vals_blocks = vals.rearrange("(n p) c -> p n c", p=P)
         q_own, q_partner = {}, {}
 
-        def load_with_halves_exchanged(tile, rows):
-            nc.sync.dma_start(tile[0:HALF, :], rows[HALF:D, :])
-            nc.sync.dma_start(tile[HALF:D, :], rows[0:HALF, :])
+        def load_with_halves_exchanged(queue, tile, rows):
+            queue.dma_start(tile[0:HALF, :], rows[HALF:D, :])
+            queue.dma_start(tile[HALF:D, :], rows[0:HALF, :])
 
         def load_keys(h):
-            nc.sync.dma_start(own_rows[h][:], kc[h * D : (h + 1) * D, :])
-            load_with_halves_exchanged(partner_rows[h], kc[h * D : (h + 1) * D, :])
+            own_rows[h] = key_pool.tile([P, S], F32, name="own_rows")
+            nc.gpsimd.dma_start(own_rows[h][:], kc[h * D : (h + 1) * D, :])
+            partner_rows[h] = key_pool.tile([P, S], F32, name="partner_rows")
+            load_with_halves_exchanged(nc.gpsimd, partner_rows[h], kc[h * D : (h + 1) * D, :])
 
         def load_q(n):
             h, b = blocks[n]
@@ -72,7 +74,7 @@ def tile_streamingattentionsink_b_kernel(tc, kc, q, vals, rc, rs, offs, out):
             q_own[n] = q_pool.tile([P, R], F32, name="q_own")
             nc.sync.dma_start(q_own[n][:], q_block)
             q_partner[n] = q_pool.tile([P, R], F32, name="q_partner")
-            load_with_halves_exchanged(q_partner[n], q_block)
+            load_with_halves_exchanged(nc.sync, q_partner[n], q_block)
 
         def load_vals(b):
             nc.sync.dma_start(vals_sb[:, b * TC : (b + 1) * TC, :], vals_blocks[:, b * TC : (b + 1) * TC, :])

@@ -10,7 +10,6 @@ U16 = mybir.dt.uint16
 MULT = mybir.AluOpType.mult
 ADD = mybir.AluOpType.add
 EXP = mybir.ActivationFunctionType.Exp
-COPY = mybir.ActivationFunctionType.Copy
 AXIS_X = mybir.AxisListType.X
 
 P = 128
@@ -28,23 +27,17 @@ def tile_streamingattentionsink_b_kernel(tc, kc, q, vals, rc, rs, offs, out):
     nc = tc.nc
     with ExitStack() as ctx:
         held = ctx.enter_context(tc.tile_pool(name="held", bufs=1))
-        key_pool = ctx.enter_context(tc.tile_pool(name="key_pool", bufs=2))
-        q_pool = ctx.enter_context(tc.tile_pool(name="q_pool", bufs=3))
         qr_pool = ctx.enter_context(tc.tile_pool(name="qr_pool", bufs=3))
-        rope_pool = ctx.enter_context(tc.tile_pool(name="rope_pool", bufs=4))
-        kr_pool = ctx.enter_context(tc.tile_pool(name="kr_pool", bufs=3))
+        rope_pool = ctx.enter_context(tc.tile_pool(name="rope_pool", bufs=3))
+        kr_pool = ctx.enter_context(tc.tile_pool(name="kr_pool", bufs=4))
         small = ctx.enter_context(tc.tile_pool(name="small", bufs=4))
-        e_pool = ctx.enter_context(tc.tile_pool(name="e_pool", bufs=2 * RC))
-        bcast_pool = ctx.enter_context(tc.tile_pool(name="bcast_pool", bufs=2))
+        e_pool = ctx.enter_context(tc.tile_pool(name="e_pool", bufs=8))
         eT_pool = ctx.enter_context(tc.tile_pool(name="eT_pool", bufs=2))
         o_pool = ctx.enter_context(tc.tile_pool(name="o_pool", bufs=2))
         ps_s = ctx.enter_context(tc.psum_pool(name="ps_s", bufs=3))
         ps_t = ctx.enter_context(tc.psum_pool(name="ps_t", bufs=3))
         ps_o = ctx.enter_context(tc.psum_pool(name="ps_o", bufs=1))
-        ps_r = ctx.enter_context(tc.psum_pool(name="ps_r", bufs=1))
-
-        blocks = [(h, b) for h in range(H) for b in range(B)]
-        NB = len(blocks)
+        ps_q = ctx.enter_context(tc.psum_pool(name="ps_q", bufs=1))
 
         offsets = held.tile([P, N // 16], U16, name="offsets")
         nc.sync.dma_start(offsets[:], offs)
@@ -52,38 +45,18 @@ def tile_streamingattentionsink_b_kernel(tc, kc, q, vals, rc, rs, offs, out):
         nc.sync.dma_start(rc_sb[:], rc)
         rs_sb = held.tile([P, T], F32, name="rs_sb")
         nc.sync.dma_start(rs_sb[:], rs)
-
-        own_rows, partner_rows = {}, {}
+        own_rows = [held.tile([P, S], F32, name=f"own_rows{h}") for h in range(H)]
+        partner_rows = [held.tile([P, S], F32, name=f"partner_rows{h}") for h in range(H)]
+        q_sb = [held.tile([P, B * R], F32, name=f"q_sb{h}") for h in range(H)]
         vals_sb = held.tile([P, N // P, H * D], BF16, name="vals_sb")
-        vals_blocks = vals.rearrange("(n p) c -> p n c", p=P)
-        q_own, q_partner = {}, {}
-
-        def load_with_halves_exchanged(queue, tile, rows):
-            queue.dma_start(tile[0:HALF, :], rows[HALF:D, :])
-            queue.dma_start(tile[HALF:D, :], rows[0:HALF, :])
-
-        def load_keys(h):
-            own_rows[h] = key_pool.tile([P, S], F32, name="own_rows")
-            nc.gpsimd.dma_start(own_rows[h][:], kc[h * D : (h + 1) * D, :])
-            partner_rows[h] = key_pool.tile([P, S], F32, name="partner_rows")
-            load_with_halves_exchanged(nc.gpsimd, partner_rows[h], kc[h * D : (h + 1) * D, :])
-
-        def load_q(n):
-            h, b = blocks[n]
-            q_block = q[h * D : (h + 1) * D, b * R : (b + 1) * R]
-            q_own[n] = q_pool.tile([P, R], F32, name="q_own")
-            nc.sync.dma_start(q_own[n][:], q_block)
-            q_partner[n] = q_pool.tile([P, R], F32, name="q_partner")
-            load_with_halves_exchanged(nc.sync, q_partner[n], q_block)
-
-        def load_vals(b):
-            nc.sync.dma_start(vals_sb[:, b * TC : (b + 1) * TC, :], vals_blocks[:, b * TC : (b + 1) * TC, :])
-
-        load_keys(0)
-        load_q(0)
-        load_q(1)
-        for b in range(B):
-            load_vals(b)
+        for h in range(H):
+            rows = kc[h * D : (h + 1) * D, :]
+            nc.sync.dma_start(own_rows[h][:], rows)
+            nc.sync.dma_start(partner_rows[h][0:HALF, :], rows[HALF:D, :])
+            nc.sync.dma_start(partner_rows[h][HALF:D, :], rows[0:HALF, :])
+            nc.sync.dma_start(q_sb[h][:], q[h * D : (h + 1) * D, :])
+            if h == 0:
+                nc.sync.dma_start(vals_sb[:], vals.rearrange("(n p) c -> p n c", p=P))
 
         ident_f = held.tile([P, P], F32, name="ident_f")
         make_identity(nc, ident_f[:])
@@ -93,67 +66,76 @@ def tile_streamingattentionsink_b_kernel(tc, kc, q, vals, rc, rs, offs, out):
         nc.vector.tensor_scalar_mul(cos_q[:], rc_sb[:, T - 1 : T], SCALE)
         sin_q = held.tile([P, 1], F32, name="sin_q")
         nc.vector.tensor_scalar_mul(sin_q[:], rs_sb[:, T - 1 : T], SCALE)
+        sin_diag = held.tile([P, P], F32, name="sin_diag")
+        nc.vector.tensor_scalar_mul(sin_diag[:], ident_f[:], sin_q[:])
+        rot = held.tile([P, P], F32, name="rot")
+        nc.vector.scalar_tensor_tensor(rot[:, 0:HALF], ident_f[:, 0:HALF], cos_q[:], sin_diag[:, HALF:D], MULT, ADD)
+        nc.vector.scalar_tensor_tensor(rot[:, HALF:D], ident_f[:, HALF:D], cos_q[:], sin_diag[:, 0:HALF], MULT, ADD)
+        rot_ps = ps_q.tile([P, P], F32, name="rot_ps", tag="q_ps")
+        nc.tensor.transpose(rot_ps[:], rot[:], ident_f[:])
+        rotT = held.tile([P, P], F32, name="rotT")
+        nc.vector.tensor_copy(rotT[:], rot_ps[:])
 
-        for n in range(NB):
-            h, b = blocks[n]
-            out_block = out[h * D : (h + 1) * D, b * R : (b + 1) * R]
-            if n + 2 < NB:
-                load_q(n + 2)
-            if b == 0 and h + 1 < H:
-                load_keys(h + 1)
+        for h in range(H):
+            for b in range(B):
+                out_block = out[h * D : (h + 1) * D, b * R : (b + 1) * R]
 
-            q_sin = qr_pool.tile([P, R], F32, name="q_sin")
-            nc.scalar.activation(q_sin[:], q_partner[n][:], COPY, scale=sin_q[:])
-            qr = qr_pool.tile([P, R], BF16, name="qr")
-            nc.vector.scalar_tensor_tensor(qr[:], q_own[n][:], cos_q[:], q_sin[:], MULT, ADD)
+                q_ps = ps_q.tile([P, R], F32, name="q_ps")
+                nc.tensor.matmul(q_ps[:], lhsT=rotT[:], rhs=q_sb[h][:, b * R : (b + 1) * R], start=True, stop=True)
+                qr = qr_pool.tile([P, R], BF16, name="qr")
+                nc.vector.tensor_copy(qr[:], q_ps[:])
 
-            piece = offsets[:, b * (T // 16) : (b + 1) * (T // 16)]
-            own = rope_pool.tile([P, T], F32, name="own")
-            nc.vector.tensor_tensor(own[:], own_rows[h][:].indirect(piece), rc_sb[:], MULT)
-            partner = rope_pool.tile([P, T], F32, name="partner")
-            nc.vector.tensor_tensor(partner[:], partner_rows[h][:].indirect(piece), rs_sb[:], MULT)
-            kr = kr_pool.tile([P, T], BF16, name="kr")
-            nc.gpsimd.tensor_tensor(kr[:], own[:], partner[:], ADD)
+                piece = offsets[:, b * (T // 16) : (b + 1) * (T // 16)]
+                own = rope_pool.tile([P, T], F32, name="own")
+                nc.vector.tensor_tensor(own[:], own_rows[h][:].indirect(piece), rc_sb[:], MULT)
+                partner = rope_pool.tile([P, T], F32, name="partner")
+                nc.vector.tensor_tensor(partner[:], partner_rows[h][:].indirect(piece), rs_sb[:], MULT)
+                kr = kr_pool.tile([P, T], BF16, name="kr")
+                nc.gpsimd.tensor_tensor(kr[:], own[:], partner[:], ADD)
 
-            negmax = small.tile([P, RC], F32, name="negmax")
-            rowsum = small.tile([P, RC], F32, name="rowsum")
-            e = []
-            for j in range(RC):
-                s_ps = ps_s.tile([P, T], F32, name="s_ps")
-                nc.tensor.matmul(s_ps[:], lhsT=qr[:, j * P : (j + 1) * P], rhs=kr[:], start=True, stop=True)
-                nc.vector.reduce_max(negmax[:, j : j + 1], s_ps[:], axis=AXIS_X, negate=True)
-                e.append(e_pool.tile([P, T], BF16, name="e"))
-                nc.scalar.activation(e[j][:], s_ps[:], EXP, bias=negmax[:, j : j + 1], accum_out=rowsum[:, j : j + 1])
+                negmax = small.tile([P, RC], F32, name="negmax")
+                rowsum = small.tile([P, RC], F32, name="rowsum")
+                e = []
+                for j in range(RC):
+                    s_ps = ps_s.tile([P, T], F32, name="s_ps")
+                    nc.tensor.matmul(s_ps[:], lhsT=qr[:, j * P : (j + 1) * P], rhs=kr[:], start=True, stop=True)
+                    nc.vector.reduce_max(negmax[:, j : j + 1], s_ps[:], axis=AXIS_X, negate=True)
+                    e.append(e_pool.tile([P, T], BF16, name="e"))
+                    nc.scalar.activation(
+                        e[j][:], s_ps[:], EXP, bias=negmax[:, j : j + 1], accum_out=rowsum[:, j : j + 1]
+                    )
 
-            rinv = small.tile([P, RC], F32, name="rinv")
-            nc.vector.reciprocal(rinv[:], rowsum[:])
-            rinvT_ps = ps_r.tile([RC, P], F32, name="rinvT_ps")
-            nc.tensor.transpose(rinvT_ps[:], rinv[:], ident_f[:])
-            rinvT = small.tile([RC, P], F32, name="rinvT")
-            nc.scalar.copy(rinvT[:], rinvT_ps[:])
-            nc.sync.dma_start(out_block[0:1, :].rearrange("o (j p) -> (o j) p", j=RC), rinvT[:])
-            rinv_bcast = bcast_pool.tile([P, R], F32, name="rinv_bcast")
-            nc.sync.dma_start(rinv_bcast[:], out_block[0, :].partition_broadcast(P))
+                rinv = small.tile([P, RC], F32, name="rinv")
+                nc.vector.reciprocal(rinv[:], rowsum[:])
+                rinvT_ps = ps_q.tile([RC, P], F32, name="rinvT_ps", tag="q_ps")
+                nc.tensor.transpose(rinvT_ps[:], rinv[:], ident_f[:])
+                rinvT = small.tile([RC, P], F32, name="rinvT")
+                nc.scalar.copy(rinvT[:], rinvT_ps[:])
+                nc.sync.dma_start(out_block[0:1, :].rearrange("o (j p) -> (o j) p", j=RC), rinvT[:])
+                rinv_bcast = o_pool.tile([P, R], F32, name="rinv_bcast")
+                nc.sync.dma_start(rinv_bcast[:], out_block[0, :].partition_broadcast(P))
 
-            eT = eT_pool.tile([P, TC, R], BF16, name="eT")
-            for pair in range(RC // 2):
-                eT_ps = ps_t.tile([P, TC, 2 * P], BF16, name="eT_ps")
-                for jj in range(2):
-                    for c in range(TC):
-                        nc.tensor.transpose(
-                            eT_ps[:, c, jj * P : (jj + 1) * P], e[2 * pair + jj][:, c * P : (c + 1) * P], ident_b[:]
-                        )
-                nc.scalar.copy(eT[:, :, pair * 2 * P : (pair + 1) * 2 * P], eT_ps[:])
+                eT = eT_pool.tile([P, TC, R], BF16, name="eT")
+                for pair in range(RC // 2):
+                    eT_ps = ps_t.tile([P, TC, 2 * P], BF16, name="eT_ps")
+                    for jj in range(2):
+                        for c in range(TC):
+                            nc.tensor.transpose(
+                                eT_ps[:, c, jj * P : (jj + 1) * P], e[2 * pair + jj][:, c * P : (c + 1) * P], ident_b[:]
+                            )
+                    nc.scalar.copy(eT[:, :, pair * 2 * P : (pair + 1) * 2 * P], eT_ps[:])
 
-            o_ps = ps_o.tile([P, R], F32, name="o_ps")
-            for c in range(TC):
-                nc.tensor.matmul(
-                    o_ps[:],
-                    lhsT=vals_sb[:, b * TC + c, h * D : (h + 1) * D],
-                    rhs=eT[:, c, :],
-                    start=(c == 0),
-                    stop=(c == TC - 1),
-                )
-            o_sb = o_pool.tile([P, R], F32, name="o_sb")
-            nc.vector.tensor_tensor(o_sb[:], o_ps[:], rinv_bcast[:], MULT)
-            nc.sync.dma_start(out_block, o_sb[:])
+                o_ps = ps_o.tile([P, R], F32, name="o_ps")
+                for c in range(TC):
+                    nc.tensor.matmul(
+                        o_ps[:],
+                        lhsT=vals_sb[:, b * TC + c, h * D : (h + 1) * D],
+                        rhs=eT[:, c, :],
+                        start=(c == 0),
+                        stop=(c == TC - 1),
+                    )
+                unscaled = o_pool.tile([P, R], F32, name="unscaled")
+                nc.scalar.copy(unscaled[:], o_ps[:])
+                o_sb = o_pool.tile([P, R], F32, name="o_sb")
+                nc.gpsimd.tensor_tensor(o_sb[:], unscaled[:], rinv_bcast[:], MULT)
+                nc.sync.dma_start(out_block, o_sb[:])

@@ -27,17 +27,25 @@ def tile_streamingattentionsink_b_kernel(tc, kc, q, vals, rc, rs, offs, out):
     nc = tc.nc
     with ExitStack() as ctx:
         held = ctx.enter_context(tc.tile_pool(name="held", bufs=1))
+        key_pool = ctx.enter_context(tc.tile_pool(name="key_pool", bufs=2))
+        q_pool = ctx.enter_context(tc.tile_pool(name="q_pool", bufs=4))
         qr_pool = ctx.enter_context(tc.tile_pool(name="qr_pool", bufs=3))
         rope_pool = ctx.enter_context(tc.tile_pool(name="rope_pool", bufs=3))
         kr_pool = ctx.enter_context(tc.tile_pool(name="kr_pool", bufs=4))
         small = ctx.enter_context(tc.tile_pool(name="small", bufs=4))
         e_pool = ctx.enter_context(tc.tile_pool(name="e_pool", bufs=8))
         eT_pool = ctx.enter_context(tc.tile_pool(name="eT_pool", bufs=2))
+        bcast_pool = ctx.enter_context(tc.tile_pool(name="bcast_pool", bufs=3))
+        u_pool = ctx.enter_context(tc.tile_pool(name="u_pool", bufs=3))
         o_pool = ctx.enter_context(tc.tile_pool(name="o_pool", bufs=2))
         ps_s = ctx.enter_context(tc.psum_pool(name="ps_s", bufs=3))
-        ps_t = ctx.enter_context(tc.psum_pool(name="ps_t", bufs=3))
+        ps_t = ctx.enter_context(tc.psum_pool(name="ps_t", bufs=2))
         ps_o = ctx.enter_context(tc.psum_pool(name="ps_o", bufs=1))
         ps_q = ctx.enter_context(tc.psum_pool(name="ps_q", bufs=1))
+        ps_r = ctx.enter_context(tc.psum_pool(name="ps_r", bufs=1))
+
+        blocks = [(h, b) for h in range(H) for b in range(B)]
+        NB = len(blocks)
 
         offsets = held.tile([P, N // 16], U16, name="offsets")
         nc.sync.dma_start(offsets[:], offs)
@@ -45,18 +53,28 @@ def tile_streamingattentionsink_b_kernel(tc, kc, q, vals, rc, rs, offs, out):
         nc.sync.dma_start(rc_sb[:], rc)
         rs_sb = held.tile([P, T], F32, name="rs_sb")
         nc.sync.dma_start(rs_sb[:], rs)
-        own_rows = [held.tile([P, S], F32, name=f"own_rows{h}") for h in range(H)]
-        partner_rows = [held.tile([P, S], F32, name=f"partner_rows{h}") for h in range(H)]
-        q_sb = [held.tile([P, B * R], F32, name=f"q_sb{h}") for h in range(H)]
         vals_sb = held.tile([P, N // P, H * D], BF16, name="vals_sb")
-        for h in range(H):
+        vals_blocks = vals.rearrange("(n p) c -> p n c", p=P)
+        own_rows, partner_rows, q_sb = {}, {}, {}
+
+        def load_keys(h):
             rows = kc[h * D : (h + 1) * D, :]
+            own_rows[h] = key_pool.tile([P, S], F32, name="own_rows")
             nc.sync.dma_start(own_rows[h][:], rows)
+            partner_rows[h] = key_pool.tile([P, S], F32, name="partner_rows")
             nc.sync.dma_start(partner_rows[h][0:HALF, :], rows[HALF:D, :])
             nc.sync.dma_start(partner_rows[h][HALF:D, :], rows[0:HALF, :])
-            nc.sync.dma_start(q_sb[h][:], q[h * D : (h + 1) * D, :])
-            if h == 0:
-                nc.sync.dma_start(vals_sb[:], vals.rearrange("(n p) c -> p n c", p=P))
+
+        def load_q(n):
+            h, b = blocks[n]
+            q_sb[n] = q_pool.tile([P, R], F32, name="q_sb")
+            nc.sync.dma_start(q_sb[n][:], q[h * D : (h + 1) * D, b * R : (b + 1) * R])
+
+        load_keys(0)
+        load_q(0)
+        load_q(1)
+        for b in range(B):
+            nc.sync.dma_start(vals_sb[:, b * TC : (b + 1) * TC, :], vals_blocks[:, b * TC : (b + 1) * TC, :])
 
         ident_f = held.tile([P, P], F32, name="ident_f")
         make_identity(nc, ident_f[:])
@@ -76,66 +94,69 @@ def tile_streamingattentionsink_b_kernel(tc, kc, q, vals, rc, rs, offs, out):
         rotT = held.tile([P, P], F32, name="rotT")
         nc.vector.tensor_copy(rotT[:], rot_ps[:])
 
-        for h in range(H):
-            for b in range(B):
-                out_block = out[h * D : (h + 1) * D, b * R : (b + 1) * R]
+        for n in range(NB):
+            h, b = blocks[n]
+            out_block = out[h * D : (h + 1) * D, b * R : (b + 1) * R]
+            if n + 2 < NB:
+                load_q(n + 2)
+            if b == 0 and h + 1 < H:
+                load_keys(h + 1)
 
-                q_ps = ps_q.tile([P, R], F32, name="q_ps")
-                nc.tensor.matmul(q_ps[:], lhsT=rotT[:], rhs=q_sb[h][:, b * R : (b + 1) * R], start=True, stop=True)
-                qr = qr_pool.tile([P, R], BF16, name="qr")
-                nc.vector.tensor_copy(qr[:], q_ps[:])
+            q_ps = ps_q.tile([P, R], F32, name="q_ps")
+            nc.tensor.matmul(q_ps[:], lhsT=rotT[:], rhs=q_sb[n][:], start=True, stop=True)
+            qr = qr_pool.tile([P, R], BF16, name="qr")
+            nc.scalar.copy(qr[:], q_ps[:])
 
-                piece = offsets[:, b * (T // 16) : (b + 1) * (T // 16)]
-                own = rope_pool.tile([P, T], F32, name="own")
-                nc.vector.tensor_tensor(own[:], own_rows[h][:].indirect(piece), rc_sb[:], MULT)
-                partner = rope_pool.tile([P, T], F32, name="partner")
-                nc.vector.tensor_tensor(partner[:], partner_rows[h][:].indirect(piece), rs_sb[:], MULT)
-                kr = kr_pool.tile([P, T], BF16, name="kr")
-                nc.gpsimd.tensor_tensor(kr[:], own[:], partner[:], ADD)
+            piece = offsets[:, b * (T // 16) : (b + 1) * (T // 16)]
+            own = rope_pool.tile([P, T], F32, name="own")
+            nc.vector.tensor_tensor(own[:], own_rows[h][:].indirect(piece), rc_sb[:], MULT)
+            partner = rope_pool.tile([P, T], F32, name="partner")
+            nc.vector.tensor_tensor(partner[:], partner_rows[h][:].indirect(piece), rs_sb[:], MULT)
+            kr = kr_pool.tile([P, T], BF16, name="kr")
+            nc.gpsimd.tensor_tensor(kr[:], own[:], partner[:], ADD)
 
-                negmax = small.tile([P, RC], F32, name="negmax")
-                rowsum = small.tile([P, RC], F32, name="rowsum")
-                e = []
-                for j in range(RC):
-                    s_ps = ps_s.tile([P, T], F32, name="s_ps")
-                    nc.tensor.matmul(s_ps[:], lhsT=qr[:, j * P : (j + 1) * P], rhs=kr[:], start=True, stop=True)
-                    nc.vector.reduce_max(negmax[:, j : j + 1], s_ps[:], axis=AXIS_X, negate=True)
-                    e.append(e_pool.tile([P, T], BF16, name="e"))
-                    nc.scalar.activation(
-                        e[j][:], s_ps[:], EXP, bias=negmax[:, j : j + 1], accum_out=rowsum[:, j : j + 1]
-                    )
+            negmax = small.tile([P, RC], F32, name="negmax")
+            rowsum = small.tile([P, RC], F32, name="rowsum")
+            e = []
+            for j in range(RC):
+                s_ps = ps_s.tile([P, T], F32, name="s_ps")
+                nc.tensor.matmul(s_ps[:], lhsT=qr[:, j * P : (j + 1) * P], rhs=kr[:], start=True, stop=True)
+                nc.vector.reduce_max(negmax[:, j : j + 1], s_ps[:], axis=AXIS_X, negate=True)
+                e.append(e_pool.tile([P, T], BF16, name="e"))
+                nc.scalar.activation(e[j][:], s_ps[:], EXP, bias=negmax[:, j : j + 1], accum_out=rowsum[:, j : j + 1])
 
-                rinv = small.tile([P, RC], F32, name="rinv")
-                nc.vector.reciprocal(rinv[:], rowsum[:])
-                rinvT_ps = ps_q.tile([RC, P], F32, name="rinvT_ps", tag="q_ps")
-                nc.tensor.transpose(rinvT_ps[:], rinv[:], ident_f[:])
-                rinvT = small.tile([RC, P], F32, name="rinvT")
-                nc.scalar.copy(rinvT[:], rinvT_ps[:])
-                nc.sync.dma_start(out_block[0:1, :].rearrange("o (j p) -> (o j) p", j=RC), rinvT[:])
-                rinv_bcast = o_pool.tile([P, R], F32, name="rinv_bcast")
-                nc.sync.dma_start(rinv_bcast[:], out_block[0, :].partition_broadcast(P))
+            rinv = small.tile([P, RC], F32, name="rinv")
+            nc.vector.reciprocal(rinv[:], rowsum[:])
+            rinvT_ps = ps_r.tile([RC, P], F32, name="rinvT_ps")
+            nc.tensor.transpose(rinvT_ps[:], rinv[:], ident_f[:])
+            rinvT = small.tile([RC, P], F32, name="rinvT")
+            nc.scalar.copy(rinvT[:], rinvT_ps[:])
+            nc.sync.dma_start(out_block[0:1, :].rearrange("o (j p) -> (o j) p", j=RC), rinvT[:])
+            rinv_bcast = bcast_pool.tile([P, R], F32, name="rinv_bcast")
+            nc.sync.dma_start(rinv_bcast[:], out_block[0, :].partition_broadcast(P))
 
-                eT = eT_pool.tile([P, TC, R], BF16, name="eT")
-                for pair in range(RC // 2):
-                    eT_ps = ps_t.tile([P, TC, 2 * P], BF16, name="eT_ps")
-                    for jj in range(2):
-                        for c in range(TC):
-                            nc.tensor.transpose(
-                                eT_ps[:, c, jj * P : (jj + 1) * P], e[2 * pair + jj][:, c * P : (c + 1) * P], ident_b[:]
-                            )
-                    nc.scalar.copy(eT[:, :, pair * 2 * P : (pair + 1) * 2 * P], eT_ps[:])
+            eT = eT_pool.tile([P, TC, R], BF16, name="eT")
+            for pair in range(RC // 2):
+                eT_ps = ps_t.tile([P, TC, 2 * P], BF16, name="eT_ps")
+                for jj in range(2):
+                    for c in range(TC):
+                        nc.tensor.transpose(
+                            eT_ps[:, c, jj * P : (jj + 1) * P], e[2 * pair + jj][:, c * P : (c + 1) * P], ident_b[:]
+                        )
+                copy_out = nc.scalar.copy if pair == 0 else nc.vector.tensor_copy
+                copy_out(eT[:, :, pair * 2 * P : (pair + 1) * 2 * P], eT_ps[:])
 
-                o_ps = ps_o.tile([P, R], F32, name="o_ps")
-                for c in range(TC):
-                    nc.tensor.matmul(
-                        o_ps[:],
-                        lhsT=vals_sb[:, b * TC + c, h * D : (h + 1) * D],
-                        rhs=eT[:, c, :],
-                        start=(c == 0),
-                        stop=(c == TC - 1),
-                    )
-                unscaled = o_pool.tile([P, R], F32, name="unscaled")
-                nc.scalar.copy(unscaled[:], o_ps[:])
-                o_sb = o_pool.tile([P, R], F32, name="o_sb")
-                nc.gpsimd.tensor_tensor(o_sb[:], unscaled[:], rinv_bcast[:], MULT)
-                nc.sync.dma_start(out_block, o_sb[:])
+            o_ps = ps_o.tile([P, R], F32, name="o_ps")
+            for c in range(TC):
+                nc.tensor.matmul(
+                    o_ps[:],
+                    lhsT=vals_sb[:, b * TC + c, h * D : (h + 1) * D],
+                    rhs=eT[:, c, :],
+                    start=(c == 0),
+                    stop=(c == TC - 1),
+                )
+            unscaled = u_pool.tile([P, R], F32, name="unscaled")
+            nc.scalar.copy(unscaled[:], o_ps[:])
+            o_sb = o_pool.tile([P, R], F32, name="o_sb")
+            nc.gpsimd.tensor_tensor(o_sb[:], unscaled[:], rinv_bcast[:], MULT)
+            nc.sync.dma_start(out_block, o_sb[:])

@@ -140,8 +140,12 @@ def tile_streamingattentionsink_b_kernel(tc, kc, q, vals, rc, rs, offs, out):
                 eT_ps = ps_t.tile([P, TC, 2 * P], BF16, name="eT_ps")
                 for jj in range(2):
                     for c in range(TC):
-                        nc.tensor.transpose(
-                            eT_ps[:, c, jj * P : (jj + 1) * P], e[2 * pair + jj][:, c * P : (c + 1) * P], ident_b[:]
+                        nc.tensor.matmul(
+                            eT_ps[:, c, jj * P : (jj + 1) * P],
+                            lhsT=e[2 * pair + jj][:, c * P : (c + 1) * P],
+                            rhs=ident_b[:],
+                            start=True,
+                            stop=True,
                         )
                 copy_out = nc.scalar.copy if pair == 0 else nc.vector.tensor_copy
                 copy_out(eT[:, :, pair * 2 * P : (pair + 1) * 2 * P], eT_ps[:])

@@ -10,7 +10,7 @@ U16 = mybir.dt.uint16
 MULT = mybir.AluOpType.mult
 ADD = mybir.AluOpType.add
 EXP = mybir.ActivationFunctionType.Exp
-AXIS_X = mybir.AxisListType.X
+COPY = mybir.ActivationFunctionType.Copy
 
 P = 128
 H, D, HALF = 4, 128, 64
@@ -19,7 +19,11 @@ S = 4096
 N = B * T
 TC = T // P
 RC = R // P
+NB = H * B
 SCALE = 1.0 / math.sqrt(D)
+VW = D + 16
+BANK = 512
+Q_AHEAD = 6
 FLOPS = 4 * H * B * T * R * D
 
 
@@ -28,24 +32,93 @@ def tile_streamingattentionsink_b_kernel(tc, kc, q, vals, rc, rs, offs, out):
     with ExitStack() as ctx:
         held = ctx.enter_context(tc.tile_pool(name="held", bufs=1))
         key_pool = ctx.enter_context(tc.tile_pool(name="key_pool", bufs=2))
-        q_pool = ctx.enter_context(tc.tile_pool(name="q_pool", bufs=4))
-        qr_pool = ctx.enter_context(tc.tile_pool(name="qr_pool", bufs=3))
-        rope_pool = ctx.enter_context(tc.tile_pool(name="rope_pool", bufs=3))
+        q_pool = ctx.enter_context(tc.tile_pool(name="q_pool", bufs=8))
+        qr_pool = ctx.enter_context(tc.tile_pool(name="qr_pool", bufs=4))
+        rope_pool = ctx.enter_context(tc.tile_pool(name="rope_pool", bufs=2))
         kr_pool = ctx.enter_context(tc.tile_pool(name="kr_pool", bufs=4))
-        small = ctx.enter_context(tc.tile_pool(name="small", bufs=4))
-        e_pool = ctx.enter_context(tc.tile_pool(name="e_pool", bufs=8))
-        eT_pool = ctx.enter_context(tc.tile_pool(name="eT_pool", bufs=2))
-        bcast_pool = ctx.enter_context(tc.tile_pool(name="bcast_pool", bufs=3))
-        u_pool = ctx.enter_context(tc.tile_pool(name="u_pool", bufs=3))
-        o_pool = ctx.enter_context(tc.tile_pool(name="o_pool", bufs=2))
-        ps_s = ctx.enter_context(tc.psum_pool(name="ps_s", bufs=3))
-        ps_t = ctx.enter_context(tc.psum_pool(name="ps_t", bufs=2))
-        ps_o = ctx.enter_context(tc.psum_pool(name="ps_o", bufs=1))
+        e_pool = ctx.enter_context(tc.tile_pool(name="e_pool", bufs=3))
+        small = ctx.enter_context(tc.tile_pool(name="small", bufs=3))
+        oT_pool = ctx.enter_context(tc.tile_pool(name="oT_pool", bufs=2))
+        o_pool = ctx.enter_context(tc.tile_pool(name="o_pool", bufs=4))
+        ps_s = ctx.enter_context(tc.psum_pool(name="ps_s", bufs=4))
+        ps_o = ctx.enter_context(tc.psum_pool(name="ps_o", bufs=2))
+        ps_t = ctx.enter_context(tc.psum_pool(name="ps_t", bufs=1))
         ps_q = ctx.enter_context(tc.psum_pool(name="ps_q", bufs=1))
-        ps_r = ctx.enter_context(tc.psum_pool(name="ps_r", bufs=1))
 
         blocks = [(h, b) for h in range(H) for b in range(B)]
-        NB = len(blocks)
+        own_rows, partner_rows, q_sb, qr, own, partner, kr, e, oT_ps, oT_sb = {}, {}, {}, {}, {}, {}, {}, {}, {}, {}
+
+        def load_head(h):
+            rows = kc[h * D : (h + 1) * D, :]
+            own_rows[h] = key_pool.tile([P, S], F32, name="own_rows")
+            nc.sync.dma_start(own_rows[h][:], rows)
+            partner_rows[h] = key_pool.tile([P, S], F32, name="partner_rows")
+            nc.sync.dma_start(partner_rows[h][0:HALF, :], rows[HALF:D, :])
+            nc.sync.dma_start(partner_rows[h][HALF:D, :], rows[0:HALF, :])
+            nc.sync.dma_start(vals_sb[:, h, :, 0:D], vals_heads[:, h, :, :])
+
+        def load_q(n):
+            h, b = blocks[n]
+            q_sb[n] = q_pool.tile([P, R], F32, name="q_sb")
+            nc.sync.dma_start(q_sb[n][:], q[h * D : (h + 1) * D, b * R : (b + 1) * R])
+
+        def rotate_queries(n):
+            q_ps = ps_q.tile([P, R], F32, name="q_ps")
+            nc.tensor.matmul(q_ps[:], lhsT=rotT[:], rhs=q_sb[n][:], start=True, stop=True)
+            qr[n] = qr_pool.tile([P, R], BF16, name="qr")
+            nc.scalar.copy(qr[n][:], q_ps[:])
+
+        def look_up_keys(n):
+            h, b = blocks[n]
+            piece = offsets[:, b * (T // 16) : (b + 1) * (T // 16)]
+            own[n] = rope_pool.tile([P, T], F32, name="own")
+            nc.vector.tensor_tensor(own[n][:], own_rows[h][:].indirect(piece), rc_sb[:], MULT)
+            partner[n] = rope_pool.tile([P, T], F32, name="partner")
+            nc.vector.tensor_tensor(partner[n][:], partner_rows[h][:].indirect(piece), rs_sb[:], MULT)
+
+        def add_halves(n):
+            kr[n] = kr_pool.tile([P, T], BF16, name="kr")
+            nc.vector.tensor_tensor(kr[n][:], own[n][:], partner[n][:], ADD)
+
+        def scores(n):
+            e[n] = e_pool.tile([P, TC, R], BF16, name="e")
+            for c in range(TC):
+                s_ps = ps_s.tile([P, R], F32, name="s_ps")
+                nc.tensor.matmul(s_ps[:], lhsT=kr[n][:, c * P : (c + 1) * P], rhs=qr[n][:], start=True, stop=True)
+                nc.scalar.activation(e[n][:, c, :], s_ps[:], EXP, scale=SCALE)
+
+        def weigh_values(n):
+            h, b = blocks[n]
+            oT_ps[n] = []
+            for pair in range(RC // 2):
+                oT_ps[n].append(ps_o.tile([P, 2, BANK // 2], F32, name="oT_ps"))
+                for jj in range(2):
+                    j = 2 * pair + jj
+                    for c in range(TC):
+                        nc.tensor.matmul(
+                            oT_ps[n][pair][:, jj, 0 : D + 1],
+                            lhsT=e[n][:, c, j * P : (j + 1) * P],
+                            rhs=vals_sb[:, h, b * TC + c, 0 : D + 1],
+                            start=(c == 0),
+                            stop=(c == TC - 1),
+                        )
+
+        def divide(n):
+            rinv = small.tile([P, RC, 1], F32, name="rinv")
+            oT_sb[n] = oT_pool.tile([P, RC, D], F32, name="oT_sb")
+            for pair in range(RC // 2):
+                nc.vector.reciprocal(rinv[:, 2 * pair : 2 * pair + 2, :], oT_ps[n][pair][:, :, D : D + 1])
+            for j in range(RC):
+                nc.scalar.activation(oT_sb[n][:, j, :], oT_ps[n][j // 2][:, j % 2, 0:D], COPY, scale=rinv[:, j, :])
+
+        def store(n):
+            h, b = blocks[n]
+            o_ps = ps_t.tile([P, R], F32, name="o_ps")
+            for j in range(RC):
+                nc.tensor.transpose(o_ps[:, j * P : (j + 1) * P], oT_sb[n][:, j, :], ident_f[:])
+            o_sb = o_pool.tile([P, R], F32, name="o_sb")
+            nc.vector.tensor_copy(o_sb[:], o_ps[:])
+            nc.sync.dma_start(out[h * D : (h + 1) * D, b * R : (b + 1) * R], o_sb[:])
 
         offsets = held.tile([P, N // 16], U16, name="offsets")
         nc.sync.dma_start(offsets[:], offs)
@@ -53,114 +126,50 @@ def tile_streamingattentionsink_b_kernel(tc, kc, q, vals, rc, rs, offs, out):
         nc.sync.dma_start(rc_sb[:], rc)
         rs_sb = held.tile([P, T], F32, name="rs_sb")
         nc.sync.dma_start(rs_sb[:], rs)
-        vals_sb = held.tile([P, N // P, H * D], BF16, name="vals_sb")
-        vals_blocks = vals.rearrange("(n p) c -> p n c", p=P)
-        own_rows, partner_rows, q_sb = {}, {}, {}
-
-        def load_keys(h):
-            rows = kc[h * D : (h + 1) * D, :]
-            own_rows[h] = key_pool.tile([P, S], F32, name="own_rows")
-            nc.sync.dma_start(own_rows[h][:], rows)
-            partner_rows[h] = key_pool.tile([P, S], F32, name="partner_rows")
-            nc.sync.dma_start(partner_rows[h][0:HALF, :], rows[HALF:D, :])
-            nc.sync.dma_start(partner_rows[h][HALF:D, :], rows[0:HALF, :])
-
-        def load_q(n):
-            h, b = blocks[n]
-            q_sb[n] = q_pool.tile([P, R], F32, name="q_sb")
-            nc.sync.dma_start(q_sb[n][:], q[h * D : (h + 1) * D, b * R : (b + 1) * R])
-
-        load_keys(0)
+        vals_sb = held.tile([P, H, N // P, VW], BF16, name="vals_sb")
+        nc.vector.memset(vals_sb[:, :, :, D:VW], 1.0)
+        vals_heads = vals.rearrange("(n p) (h d) -> p h n d", p=P, h=H)
         load_q(0)
-        load_q(1)
-        for b in range(B):
-            nc.sync.dma_start(vals_sb[:, b * TC : (b + 1) * TC, :], vals_blocks[:, b * TC : (b + 1) * TC, :])
+        load_head(0)
+        for n in range(1, Q_AHEAD):
+            load_q(n)
+        load_head(1)
 
         ident_f = held.tile([P, P], F32, name="ident_f")
         make_identity(nc, ident_f[:])
-        ident_b = held.tile([P, P], BF16, name="ident_b")
-        nc.vector.tensor_copy(ident_b[:], ident_f[:])
-        cos_q = held.tile([P, 1], F32, name="cos_q")
-        nc.vector.tensor_scalar_mul(cos_q[:], rc_sb[:, T - 1 : T], SCALE)
-        sin_q = held.tile([P, 1], F32, name="sin_q")
-        nc.vector.tensor_scalar_mul(sin_q[:], rs_sb[:, T - 1 : T], SCALE)
+        cos_q = rc_sb[:, T - 1 : T]
+        sin_q = rs_sb[:, T - 1 : T]
         sin_diag = held.tile([P, P], F32, name="sin_diag")
-        nc.vector.tensor_scalar_mul(sin_diag[:], ident_f[:], sin_q[:])
+        nc.vector.tensor_scalar_mul(sin_diag[:], ident_f[:], sin_q)
         rot = held.tile([P, P], F32, name="rot")
-        nc.vector.scalar_tensor_tensor(rot[:, 0:HALF], ident_f[:, 0:HALF], cos_q[:], sin_diag[:, HALF:D], MULT, ADD)
-        nc.vector.scalar_tensor_tensor(rot[:, HALF:D], ident_f[:, HALF:D], cos_q[:], sin_diag[:, 0:HALF], MULT, ADD)
+        nc.vector.scalar_tensor_tensor(rot[:, 0:HALF], ident_f[:, 0:HALF], cos_q, sin_diag[:, HALF:D], MULT, ADD)
+        nc.vector.scalar_tensor_tensor(rot[:, HALF:D], ident_f[:, HALF:D], cos_q, sin_diag[:, 0:HALF], MULT, ADD)
         rot_ps = ps_q.tile([P, P], F32, name="rot_ps", tag="q_ps")
         nc.tensor.transpose(rot_ps[:], rot[:], ident_f[:])
         rotT = held.tile([P, P], F32, name="rotT")
         nc.vector.tensor_copy(rotT[:], rot_ps[:])
 
-        for n in range(NB):
-            h, b = blocks[n]
-            out_block = out[h * D : (h + 1) * D, b * R : (b + 1) * R]
-            if n + 2 < NB:
-                load_q(n + 2)
-            if b == 0 and h + 1 < H:
-                load_keys(h + 1)
-
-            q_ps = ps_q.tile([P, R], F32, name="q_ps")
-            nc.tensor.matmul(q_ps[:], lhsT=rotT[:], rhs=q_sb[n][:], start=True, stop=True)
-            qr = qr_pool.tile([P, R], BF16, name="qr")
-            nc.scalar.copy(qr[:], q_ps[:])
-
-            piece = offsets[:, b * (T // 16) : (b + 1) * (T // 16)]
-            own = rope_pool.tile([P, T], F32, name="own")
-            nc.vector.tensor_tensor(own[:], own_rows[h][:].indirect(piece), rc_sb[:], MULT)
-            partner = rope_pool.tile([P, T], F32, name="partner")
-            nc.vector.tensor_tensor(partner[:], partner_rows[h][:].indirect(piece), rs_sb[:], MULT)
-            kr = kr_pool.tile([P, T], BF16, name="kr")
-            nc.gpsimd.tensor_tensor(kr[:], own[:], partner[:], ADD)
-
-            negmax = small.tile([P, RC], F32, name="negmax")
-            rowsum = small.tile([P, RC], F32, name="rowsum")
-            e = []
-            for j in range(RC):
-                s_ps = ps_s.tile([P, T], F32, name="s_ps")
-                nc.tensor.matmul(s_ps[:], lhsT=qr[:, j * P : (j + 1) * P], rhs=kr[:], start=True, stop=True)
-                nc.vector.reduce_max(negmax[:, j : j + 1], s_ps[:], axis=AXIS_X, negate=True)
-                e.append(e_pool.tile([P, T], BF16, name="e"))
-                nc.scalar.activation(e[j][:], s_ps[:], EXP, bias=negmax[:, j : j + 1], accum_out=rowsum[:, j : j + 1])
-
-            rinv = small.tile([P, RC], F32, name="rinv")
-            nc.vector.reciprocal(rinv[:], rowsum[:])
-            rinvT_ps = ps_r.tile([RC, P], F32, name="rinvT_ps")
-            nc.tensor.transpose(rinvT_ps[:], rinv[:], ident_f[:])
-            rinvT = small.tile([RC, P], F32, name="rinvT")
-            nc.scalar.copy(rinvT[:], rinvT_ps[:])
-            nc.sync.dma_start(out_block[0:1, :].rearrange("o (j p) -> (o j) p", j=RC), rinvT[:])
-            rinv_bcast = bcast_pool.tile([P, R], F32, name="rinv_bcast")
-            nc.sync.dma_start(rinv_bcast[:], out_block[0, :].partition_broadcast(P))
-
-            eT = eT_pool.tile([P, TC, R], BF16, name="eT")
-            for pair in range(RC // 2):
-                eT_ps = ps_t.tile([P, TC, 2 * P], BF16, name="eT_ps")
-                for jj in range(2):
-                    for c in range(TC):
-                        nc.tensor.matmul(
-                            eT_ps[:, c, jj * P : (jj + 1) * P],
-                            lhsT=e[2 * pair + jj][:, c * P : (c + 1) * P],
-                            rhs=ident_b[:],
-                            start=True,
-                            stop=True,
-                        )
-                copy_out = nc.scalar.copy if pair == 0 else nc.vector.tensor_copy
-                copy_out(eT[:, :, pair * 2 * P : (pair + 1) * 2 * P], eT_ps[:])
-
-            o_ps = ps_o.tile([P, R], F32, name="o_ps")
-            for c in range(TC):
-                nc.tensor.matmul(
-                    o_ps[:],
-                    lhsT=vals_sb[:, b * TC + c, h * D : (h + 1) * D],
-                    rhs=eT[:, c, :],
-                    start=(c == 0),
-                    stop=(c == TC - 1),
-                )
-            unscaled = u_pool.tile([P, R], F32, name="unscaled")
-            nc.scalar.copy(unscaled[:], o_ps[:])
-            o_sb = o_pool.tile([P, R], F32, name="o_sb")
-            nc.gpsimd.tensor_tensor(o_sb[:], unscaled[:], rinv_bcast[:], MULT)
-            nc.sync.dma_start(out_block, o_sb[:])
+        for n in range(2):
+            rotate_queries(n)
+            look_up_keys(n)
+            add_halves(n)
+        for i in range(NB + 2):
+            ahead = i + 2
+            if 0 <= i - 2:
+                divide(i - 2)
+            if i < NB:
+                scores(i)
+            if ahead < NB:
+                if i + Q_AHEAD < NB:
+                    load_q(i + Q_AHEAD)
+                h, b = blocks[ahead]
+                if b == 0 and 1 <= h < H - 1:
+                    load_head(h + 1)
+                look_up_keys(ahead)
+                rotate_queries(ahead)
+            if 0 <= i - 2:
+                store(i - 2)
+            if ahead < NB:
+                add_halves(ahead)
+            if 0 <= i - 1 < NB:
+                weigh_values(i - 1)

@@ -23,7 +23,6 @@ NB = H * B
 SCALE = 1.0 / math.sqrt(D)
 VW = D + 16
 BANK = 512
-Q_AHEAD = 6
 FLOPS = 4 * H * B * T * R * D
 
 
@@ -31,36 +30,42 @@ def tile_streamingattentionsink_b_kernel(tc, kc, q, vals, rc, rs, offs, out):
     nc = tc.nc
     with ExitStack() as ctx:
         held = ctx.enter_context(tc.tile_pool(name="held", bufs=1))
-        key_pool = ctx.enter_context(tc.tile_pool(name="key_pool", bufs=2))
-        q_pool = ctx.enter_context(tc.tile_pool(name="q_pool", bufs=8))
+        key_pool = ctx.enter_context(tc.tile_pool(name="key_pool", bufs=H))
+        q_pool = ctx.enter_context(tc.tile_pool(name="q_pool", bufs=NB))
         qr_pool = ctx.enter_context(tc.tile_pool(name="qr_pool", bufs=4))
         rope_pool = ctx.enter_context(tc.tile_pool(name="rope_pool", bufs=2))
         kr_pool = ctx.enter_context(tc.tile_pool(name="kr_pool", bufs=4))
         e_pool = ctx.enter_context(tc.tile_pool(name="e_pool", bufs=3))
         small = ctx.enter_context(tc.tile_pool(name="small", bufs=3))
         oT_pool = ctx.enter_context(tc.tile_pool(name="oT_pool", bufs=2))
-        o_pool = ctx.enter_context(tc.tile_pool(name="o_pool", bufs=4))
+        o_pool = ctx.enter_context(tc.tile_pool(name="o_pool", bufs=6))
         ps_s = ctx.enter_context(tc.psum_pool(name="ps_s", bufs=4))
         ps_o = ctx.enter_context(tc.psum_pool(name="ps_o", bufs=2))
         ps_t = ctx.enter_context(tc.psum_pool(name="ps_t", bufs=1))
         ps_q = ctx.enter_context(tc.psum_pool(name="ps_q", bufs=1))
 
         blocks = [(h, b) for h in range(H) for b in range(B)]
-        own_rows, partner_rows, q_sb, qr, own, partner, kr, e, oT_ps, oT_sb = {}, {}, {}, {}, {}, {}, {}, {}, {}, {}
+        own_rows, partner_rows, vals_sb, q_sb, qr, own, partner, kr, e, oT_ps, oT_sb = {}, {}, {}, {}, {}, {}, {}, {}, {}, {}, {}
+
+        def load_channels(tile, on_even, on_odd):
+            nc.sync.dma_start(tile[0:P:2, :], on_even)
+            nc.sync.dma_start(tile[1:P:2, :], on_odd)
 
         def load_head(h):
             rows = kc[h * D : (h + 1) * D, :]
             own_rows[h] = key_pool.tile([P, S], F32, name="own_rows")
-            nc.sync.dma_start(own_rows[h][:], rows)
+            load_channels(own_rows[h], rows[0:HALF, :], rows[HALF:D, :])
             partner_rows[h] = key_pool.tile([P, S], F32, name="partner_rows")
-            nc.sync.dma_start(partner_rows[h][0:HALF, :], rows[HALF:D, :])
-            nc.sync.dma_start(partner_rows[h][HALF:D, :], rows[0:HALF, :])
-            nc.sync.dma_start(vals_sb[:, h, :, 0:D], vals_heads[:, h, :, :])
+            load_channels(partner_rows[h], rows[HALF:D, :], rows[0:HALF, :])
+            vals_sb[h] = held.tile([P, N // P, VW], BF16, name="vals_sb%d" % h)
+            nc.gpsimd.memset(vals_sb[h][:, :, D:VW], 1.0)
+            nc.sync.dma_start(vals_sb[h][:, :, 0:D], vals_heads[:, h, :, :])
 
         def load_q(n):
             h, b = blocks[n]
             q_sb[n] = q_pool.tile([P, R], F32, name="q_sb")
-            nc.sync.dma_start(q_sb[n][:], q[h * D : (h + 1) * D, b * R : (b + 1) * R])
+            columns = slice(b * R, (b + 1) * R)
+            load_channels(q_sb[n], q[h * D : h * D + HALF, columns], q[h * D + HALF : (h + 1) * D, columns])
 
         def rotate_queries(n):
             q_ps = ps_q.tile([P, R], F32, name="q_ps")
@@ -98,7 +103,7 @@ def tile_streamingattentionsink_b_kernel(tc, kc, q, vals, rc, rs, offs, out):
                         nc.tensor.matmul(
                             oT_ps[n][pair][:, jj, 0 : D + 1],
                             lhsT=e[n][:, c, j * P : (j + 1) * P],
-                            rhs=vals_sb[:, h, b * TC + c, 0 : D + 1],
+                            rhs=vals_sb[h][:, b * TC + c, 0 : D + 1],
                             start=(c == 0),
                             stop=(c == TC - 1),
                         )
@@ -123,17 +128,18 @@ def tile_streamingattentionsink_b_kernel(tc, kc, q, vals, rc, rs, offs, out):
         offsets = held.tile([P, N // 16], U16, name="offsets")
         nc.sync.dma_start(offsets[:], offs)
         rc_sb = held.tile([P, T], F32, name="rc_sb")
-        nc.sync.dma_start(rc_sb[:], rc)
+        load_channels(rc_sb, rc[0:HALF, :], rc[HALF:D, :])
         rs_sb = held.tile([P, T], F32, name="rs_sb")
-        nc.sync.dma_start(rs_sb[:], rs)
-        vals_sb = held.tile([P, H, N // P, VW], BF16, name="vals_sb")
-        nc.vector.memset(vals_sb[:, :, :, D:VW], 1.0)
+        load_channels(rs_sb, rs[0:HALF, :], rs[HALF:D, :])
         vals_heads = vals.rearrange("(n p) (h d) -> p h n d", p=P, h=H)
         load_q(0)
         load_head(0)
-        for n in range(1, Q_AHEAD):
-            load_q(n)
-        load_head(1)
+        for h in range(1, H):
+            for n in range(B * (h - 1) + 2 - (h == 1), B * h + 2):
+                load_q(n)
+            load_head(h)
+        load_q(NB - 2)
+        load_q(NB - 1)
 
         ident_f = held.tile([P, P], F32, name="ident_f")
         make_identity(nc, ident_f[:])
@@ -142,8 +148,8 @@ def tile_streamingattentionsink_b_kernel(tc, kc, q, vals, rc, rs, offs, out):
         sin_diag = held.tile([P, P], F32, name="sin_diag")
         nc.vector.tensor_scalar_mul(sin_diag[:], ident_f[:], sin_q)
         rot = held.tile([P, P], F32, name="rot")
-        nc.vector.scalar_tensor_tensor(rot[:, 0:HALF], ident_f[:, 0:HALF], cos_q, sin_diag[:, HALF:D], MULT, ADD)
-        nc.vector.scalar_tensor_tensor(rot[:, HALF:D], ident_f[:, HALF:D], cos_q, sin_diag[:, 0:HALF], MULT, ADD)
+        nc.vector.scalar_tensor_tensor(rot[:, 0:P:2], ident_f[:, 0:P:2], cos_q, sin_diag[:, 1:P:2], MULT, ADD)
+        nc.vector.scalar_tensor_tensor(rot[:, 1:P:2], ident_f[:, 1:P:2], cos_q, sin_diag[:, 0:P:2], MULT, ADD)
         rot_ps = ps_q.tile([P, P], F32, name="rot_ps", tag="q_ps")
         nc.tensor.transpose(rot_ps[:], rot[:], ident_f[:])
         rotT = held.tile([P, P], F32, name="rotT")
@@ -160,11 +166,6 @@ def tile_streamingattentionsink_b_kernel(tc, kc, q, vals, rc, rs, offs, out):
             if i < NB:
                 scores(i)
             if ahead < NB:
-                if i + Q_AHEAD < NB:
-                    load_q(i + Q_AHEAD)
-                h, b = blocks[ahead]
-                if b == 0 and 1 <= h < H - 1:
-                    load_head(h + 1)
                 look_up_keys(ahead)
                 rotate_queries(ahead)
             if 0 <= i - 2:

@@ -49,7 +49,7 @@ def tile_streamingattentionsink_b_kernel(tc, kc, q, vals, rc, rs, offs, out):
 
         def load_channels(tile, on_even, on_odd):
             nc.sync.dma_start(tile[0:P:2, :], on_even)
-            nc.sync.dma_start(tile[1:P:2, :], on_odd)
+            nc.gpsimd.dma_start(tile[1:P:2, :], on_odd)
 
         def load_head(h):
             rows = kc[h * D : (h + 1) * D, :]
@@ -125,6 +125,9 @@ def tile_streamingattentionsink_b_kernel(tc, kc, q, vals, rc, rs, offs, out):
             nc.vector.tensor_copy(o_sb[:], o_ps[:])
             nc.sync.dma_start(out[h * D : (h + 1) * D, b * R : (b + 1) * R], o_sb[:])
 
+        ident_f = held.tile([P, P], F32, name="ident_f")
+        make_identity(nc, ident_f[:])
+
         offsets = held.tile([P, N // 16], U16, name="offsets")
         nc.sync.dma_start(offsets[:], offs)
         rc_sb = held.tile([P, T], F32, name="rc_sb")
@@ -141,8 +144,6 @@ def tile_streamingattentionsink_b_kernel(tc, kc, q, vals, rc, rs, offs, out):
         load_q(NB - 2)
         load_q(NB - 1)
 
-        ident_f = held.tile([P, P], F32, name="ident_f")
-        make_identity(nc, ident_f[:])
         cos_q = rc_sb[:, T - 1 : T]
         sin_q = rs_sb[:, T - 1 : T]
         sin_diag = held.tile([P, P], F32, name="sin_diag")

@@ -31,9 +31,9 @@ def tile_streamingattentionsink_b_kernel(tc, kc, q, vals, rc, rs, offs, out):
     with ExitStack() as ctx:
         held = ctx.enter_context(tc.tile_pool(name="held", bufs=1))
         key_pool = ctx.enter_context(tc.tile_pool(name="key_pool", bufs=H))
-        q_pool = ctx.enter_context(tc.tile_pool(name="q_pool", bufs=NB))
+        q_pool = ctx.enter_context(tc.tile_pool(name="q_pool", bufs=H))
         qr_pool = ctx.enter_context(tc.tile_pool(name="qr_pool", bufs=4))
-        rope_pool = ctx.enter_context(tc.tile_pool(name="rope_pool", bufs=2))
+        rope_pool = ctx.enter_context(tc.tile_pool(name="rope_pool", bufs=3))
         kr_pool = ctx.enter_context(tc.tile_pool(name="kr_pool", bufs=4))
         e_pool = ctx.enter_context(tc.tile_pool(name="e_pool", bufs=3))
         small = ctx.enter_context(tc.tile_pool(name="small", bufs=3))
@@ -45,45 +45,38 @@ def tile_streamingattentionsink_b_kernel(tc, kc, q, vals, rc, rs, offs, out):
         ps_q = ctx.enter_context(tc.psum_pool(name="ps_q", bufs=1))
 
         blocks = [(h, b) for h in range(H) for b in range(B)]
-        own_rows, partner_rows, vals_sb, q_sb, qr, own, partner, kr, e, oT_ps, oT_sb = {}, {}, {}, {}, {}, {}, {}, {}, {}, {}, {}
-
-        def load_channels(tile, on_even, on_odd):
-            nc.sync.dma_start(tile[0:P:2, :], on_even)
-            nc.gpsimd.dma_start(tile[1:P:2, :], on_odd)
+        keys, queries, vals_sb, qr, own, crossed, moved, kr, e, oT_ps, oT_sb = {}, {}, {}, {}, {}, {}, {}, {}, {}, {}, {}
 
         def load_head(h):
-            rows = kc[h * D : (h + 1) * D, :]
-            own_rows[h] = key_pool.tile([P, S], F32, name="own_rows")
-            load_channels(own_rows[h], rows[0:HALF, :], rows[HALF:D, :])
-            partner_rows[h] = key_pool.tile([P, S], F32, name="partner_rows")
-            load_channels(partner_rows[h], rows[HALF:D, :], rows[0:HALF, :])
+            keys[h] = key_pool.tile([P, S], F32, name="keys")
+            nc.sync.dma_start(keys[h][:], kc[h * D : (h + 1) * D, :])
+            queries[h] = q_pool.tile([P, B * R], F32, name="queries")
+            nc.sync.dma_start(queries[h][:], q[h * D : (h + 1) * D, :])
             vals_sb[h] = held.tile([P, N // P, VW], BF16, name="vals_sb%d" % h)
             nc.gpsimd.memset(vals_sb[h][:, :, D:VW], 1.0)
             nc.sync.dma_start(vals_sb[h][:, :, 0:D], vals_heads[:, h, :, :])
 
-        def load_q(n):
-            h, b = blocks[n]
-            q_sb[n] = q_pool.tile([P, R], F32, name="q_sb")
-            columns = slice(b * R, (b + 1) * R)
-            load_channels(q_sb[n], q[h * D : h * D + HALF, columns], q[h * D + HALF : (h + 1) * D, columns])
-
         def rotate_queries(n):
+            h, b = blocks[n]
             q_ps = ps_q.tile([P, R], F32, name="q_ps")
-            nc.tensor.matmul(q_ps[:], lhsT=rotT[:], rhs=q_sb[n][:], start=True, stop=True)
+            nc.tensor.matmul(q_ps[:], lhsT=rotT[:], rhs=queries[h][:, b * R : (b + 1) * R], start=True, stop=True)
             qr[n] = qr_pool.tile([P, R], BF16, name="qr")
             nc.scalar.copy(qr[n][:], q_ps[:])
 
         def look_up_keys(n):
             h, b = blocks[n]
             piece = offsets[:, b * (T // 16) : (b + 1) * (T // 16)]
+            crossed[n] = rope_pool.tile([P, T], F32, name="crossed")
+            nc.vector.tensor_tensor(crossed[n][:], keys[h][:].indirect(piece), rs_partner[:], MULT)
+            moved[n] = rope_pool.tile([P, T], F32, name="moved")
+            nc.gpsimd.dma_start(moved[n][0:HALF, :], crossed[n][HALF:P, :])
+            nc.gpsimd.dma_start(moved[n][HALF:P, :], crossed[n][0:HALF, :])
             own[n] = rope_pool.tile([P, T], F32, name="own")
-            nc.vector.tensor_tensor(own[n][:], own_rows[h][:].indirect(piece), rc_sb[:], MULT)
-            partner[n] = rope_pool.tile([P, T], F32, name="partner")
-            nc.vector.tensor_tensor(partner[n][:], partner_rows[h][:].indirect(piece), rs_sb[:], MULT)
+            nc.vector.tensor_tensor(own[n][:], keys[h][:].indirect(piece), rc_sb[:], MULT)
 
         def add_halves(n):
             kr[n] = kr_pool.tile([P, T], BF16, name="kr")
-            nc.vector.tensor_tensor(kr[n][:], own[n][:], partner[n][:], ADD)
+            nc.vector.tensor_tensor(kr[n][:], own[n][:], moved[n][:], ADD)
 
         def scores(n):
             e[n] = e_pool.tile([P, TC, R], BF16, name="e")
@@ -131,47 +124,39 @@ def tile_streamingattentionsink_b_kernel(tc, kc, q, vals, rc, rs, offs, out):
         offsets = held.tile([P, N // 16], U16, name="offsets")
         nc.sync.dma_start(offsets[:], offs)
         rc_sb = held.tile([P, T], F32, name="rc_sb")
-        load_channels(rc_sb, rc[0:HALF, :], rc[HALF:D, :])
-        rs_sb = held.tile([P, T], F32, name="rs_sb")
-        load_channels(rs_sb, rs[0:HALF, :], rs[HALF:D, :])
+        nc.sync.dma_start(rc_sb[:], rc)
+        rs_partner = held.tile([P, T], F32, name="rs_partner")
+        nc.sync.dma_start(rs_partner[0:HALF, :], rs[HALF:D, :])
+        nc.sync.dma_start(rs_partner[HALF:D, :], rs[0:HALF, :])
         vals_heads = vals.rearrange("(n p) (h d) -> p h n d", p=P, h=H)
-        load_q(0)
-        load_head(0)
-        for h in range(1, H):
-            for n in range(B * (h - 1) + 2 - (h == 1), B * h + 2):
-                load_q(n)
+        for h in range(H):
             load_head(h)
-        load_q(NB - 2)
-        load_q(NB - 1)
 
         cos_q = rc_sb[:, T - 1 : T]
-        sin_q = rs_sb[:, T - 1 : T]
+        sin_q = rs_partner[:, T - 1 : T]
         sin_diag = held.tile([P, P], F32, name="sin_diag")
         nc.vector.tensor_scalar_mul(sin_diag[:], ident_f[:], sin_q)
-        rot = held.tile([P, P], F32, name="rot")
-        nc.vector.scalar_tensor_tensor(rot[:, 0:P:2], ident_f[:, 0:P:2], cos_q, sin_diag[:, 1:P:2], MULT, ADD)
-        nc.vector.scalar_tensor_tensor(rot[:, 1:P:2], ident_f[:, 1:P:2], cos_q, sin_diag[:, 0:P:2], MULT, ADD)
-        rot_ps = ps_q.tile([P, P], F32, name="rot_ps", tag="q_ps")
-        nc.tensor.transpose(rot_ps[:], rot[:], ident_f[:])
         rotT = held.tile([P, P], F32, name="rotT")
-        nc.vector.tensor_copy(rotT[:], rot_ps[:])
+        nc.vector.scalar_tensor_tensor(rotT[:, 0:HALF], ident_f[:, 0:HALF], cos_q, sin_diag[:, HALF:P], MULT, ADD)
+        nc.vector.scalar_tensor_tensor(rotT[:, HALF:P], ident_f[:, HALF:P], cos_q, sin_diag[:, 0:HALF], MULT, ADD)
 
+        for n in range(3):
+            look_up_keys(n)
         for n in range(2):
             rotate_queries(n)
-            look_up_keys(n)
             add_halves(n)
         for i in range(NB + 2):
-            ahead = i + 2
             if 0 <= i - 2:
                 divide(i - 2)
             if i < NB:
                 scores(i)
-            if ahead < NB:
-                look_up_keys(ahead)
-                rotate_queries(ahead)
+            if i + 3 < NB:
+                look_up_keys(i + 3)
+            if i + 2 < NB:
+                rotate_queries(i + 2)
             if 0 <= i - 2:
                 store(i - 2)
-            if ahead < NB:
-                add_halves(ahead)
+            if i + 2 < NB:
+                add_halves(i + 2)
             if 0 <= i - 1 < NB:
                 weigh_values(i - 1)

@@ -22,6 +22,7 @@ RC = R // P
 NB = H * B
 SCALE = 1.0 / math.sqrt(D)
 VW = D + 16
+PIECE = 512
 BANK = 512
 FLOPS = 4 * H * B * T * R * D
 
@@ -30,10 +31,12 @@ def tile_streamingattentionsink_b_kernel(tc, kc, q, vals, rc, rs, offs, out):
     nc = tc.nc
     with ExitStack() as ctx:
         held = ctx.enter_context(tc.tile_pool(name="held", bufs=1))
-        key_pool = ctx.enter_context(tc.tile_pool(name="key_pool", bufs=H))
-        q_pool = ctx.enter_context(tc.tile_pool(name="q_pool", bufs=H))
+        key_pool = ctx.enter_context(tc.tile_pool(name="key_pool", bufs=2))
+        q_pool = ctx.enter_context(tc.tile_pool(name="q_pool", bufs=B))
+        vals_pool = ctx.enter_context(tc.tile_pool(name="vals_pool", bufs=2))
         qr_pool = ctx.enter_context(tc.tile_pool(name="qr_pool", bufs=4))
-        rope_pool = ctx.enter_context(tc.tile_pool(name="rope_pool", bufs=3))
+        own_pool = ctx.enter_context(tc.tile_pool(name="own_pool", bufs=3))
+        swap_pool = ctx.enter_context(tc.tile_pool(name="swap_pool", bufs=3))
         kr_pool = ctx.enter_context(tc.tile_pool(name="kr_pool", bufs=4))
         e_pool = ctx.enter_context(tc.tile_pool(name="e_pool", bufs=3))
         small = ctx.enter_context(tc.tile_pool(name="small", bufs=3))
@@ -45,45 +48,63 @@ def tile_streamingattentionsink_b_kernel(tc, kc, q, vals, rc, rs, offs, out):
         ps_q = ctx.enter_context(tc.psum_pool(name="ps_q", bufs=1))
 
         blocks = [(h, b) for h in range(H) for b in range(B)]
-        keys, queries, vals_sb, qr, own, crossed, moved, kr, e, oT_ps, oT_sb = {}, {}, {}, {}, {}, {}, {}, {}, {}, {}, {}
+        keys, crossed, moved, own, kr, queries, q_ps, qr = {}, {}, {}, {}, {}, {}, {}, {}
+        vals_sb, s_ps, e, oT_ps, rinv, oT_sb, o_ps = {}, {}, {}, {}, {}, {}, {}
 
         def load_head(h):
             keys[h] = key_pool.tile([P, S], F32, name="keys")
-            nc.sync.dma_start(keys[h][:], kc[h * D : (h + 1) * D, :])
-            queries[h] = q_pool.tile([P, B * R], F32, name="queries")
-            nc.sync.dma_start(queries[h][:], q[h * D : (h + 1) * D, :])
-            vals_sb[h] = held.tile([P, N // P, VW], BF16, name="vals_sb%d" % h)
+            for s in range(0, S, PIECE):
+                nc.sync.dma_start(keys[h][:, s : s + PIECE], kc[h * D : (h + 1) * D, s : s + PIECE])
+            vals_sb[h] = vals_pool.tile([P, N // P, VW], BF16, name="vals_sb")
             nc.gpsimd.memset(vals_sb[h][:, :, D:VW], 1.0)
             nc.sync.dma_start(vals_sb[h][:, :, 0:D], vals_heads[:, h, :, :])
 
+        def load_queries(n):
+            h, b = blocks[n]
+            queries[n] = q_pool.tile([P, R], F32, name="queries")
+            nc.sync.dma_start(queries[n][:], q[h * D : (h + 1) * D, b * R : (b + 1) * R])
+
         def rotate_queries(n):
-            h, b = blocks[n]
-            q_ps = ps_q.tile([P, R], F32, name="q_ps")
-            nc.tensor.matmul(q_ps[:], lhsT=rotT[:], rhs=queries[h][:, b * R : (b + 1) * R], start=True, stop=True)
+            q_ps[n] = ps_q.tile([P, R], F32, name="q_ps")
+            nc.tensor.matmul(q_ps[n][:], lhsT=rotT[:], rhs=queries[n][:], start=True, stop=True)
+
+        def round_queries(n):
             qr[n] = qr_pool.tile([P, R], BF16, name="qr")
-            nc.scalar.copy(qr[n][:], q_ps[:])
+            nc.scalar.copy(qr[n][:], q_ps[n][:])
 
-        def look_up_keys(n):
+        def piece(b):
+            return offsets[:, b * (T // 16) : (b + 1) * (T // 16)]
+
+        def look_up_partners(n):
             h, b = blocks[n]
-            piece = offsets[:, b * (T // 16) : (b + 1) * (T // 16)]
-            crossed[n] = rope_pool.tile([P, T], F32, name="crossed")
-            nc.vector.tensor_tensor(crossed[n][:], keys[h][:].indirect(piece), rs_partner[:], MULT)
-            moved[n] = rope_pool.tile([P, T], F32, name="moved")
-            nc.gpsimd.dma_start(moved[n][0:HALF, :], crossed[n][HALF:P, :])
-            nc.gpsimd.dma_start(moved[n][HALF:P, :], crossed[n][0:HALF, :])
-            own[n] = rope_pool.tile([P, T], F32, name="own")
-            nc.vector.tensor_tensor(own[n][:], keys[h][:].indirect(piece), rc_sb[:], MULT)
+            g, place = (n + 1) // 2, (n + 1) % 2
+            if n == 0 or place == 0:
+                crossed[g] = swap_pool.tile([P, 2, T], F32, name="crossed")
+                moved[g] = swap_pool.tile([P, 2, T], F32, name="moved")
+            nc.vector.tensor_tensor(crossed[g][:, place, :], keys[h][:].indirect(piece(b)), rs_partner[:], MULT)
+            if place == 1 or n == NB - 1:
+                used = slice(1, 2) if n == 0 else slice(0, place + 1)
+                nc.sync.dma_start(moved[g][0:HALF, used, :], crossed[g][HALF:P, used, :])
+                nc.gpsimd.dma_start(moved[g][HALF:P, used, :], crossed[g][0:HALF, used, :])
 
-        def add_halves(n):
+        def look_up_own(n):
+            h, b = blocks[n]
+            own[n] = own_pool.tile([P, T], F32, name="own")
+            nc.vector.tensor_tensor(own[n][:], keys[h][:].indirect(piece(b)), rc_sb[:], MULT)
+
+        def add_terms(n):
             kr[n] = kr_pool.tile([P, T], BF16, name="kr")
-            nc.vector.tensor_tensor(kr[n][:], own[n][:], moved[n][:], ADD)
+            nc.vector.tensor_tensor(kr[n][:], own[n][:], moved[(n + 1) // 2][:, (n + 1) % 2, :], ADD)
 
         def scores(n):
+            s_ps[n] = [ps_s.tile([P, R], F32, name="s_ps") for _ in range(TC)]
+            for c in range(TC):
+                nc.tensor.matmul(s_ps[n][c][:], lhsT=kr[n][:, c * P : (c + 1) * P], rhs=qr[n][:], start=True, stop=True)
+
+        def exponentials(n):
             e[n] = e_pool.tile([P, TC, R], BF16, name="e")
             for c in range(TC):
-                s_ps = ps_s.tile([P, R], F32, name="s_ps")
-                nc.tensor.matmul(s_ps[:], lhsT=kr[n][:, c * P : (c + 1) * P], rhs=qr[n][:], start=True, stop=True)
-                nc.scalar.activation(e[n][:, c, :], s_ps[:], EXP, scale=SCALE)
+                nc.scalar.activation(e[n][:, c, :], s_ps[n][c][:], EXP, scale=SCALE)
 
         def weigh_values(n):
             h, b = blocks[n]
@@ -101,21 +122,25 @@ def tile_streamingattentionsink_b_kernel(tc, kc, q, vals, rc, rs, offs, out):
                             stop=(c == TC - 1),
                         )
 
-        def divide(n):
-            rinv = small.tile([P, RC, 1], F32, name="rinv")
-            oT_sb[n] = oT_pool.tile([P, RC, D], F32, name="oT_sb")
+        def invert_sums(n):
+            rinv[n] = small.tile([P, RC, 1], F32, name="rinv")
             for pair in range(RC // 2):
-                nc.vector.reciprocal(rinv[:, 2 * pair : 2 * pair + 2, :], oT_ps[n][pair][:, :, D : D + 1])
+                nc.vector.reciprocal(rinv[n][:, 2 * pair : 2 * pair + 2, :], oT_ps[n][pair][:, :, D : D + 1])
+
+        def divide(n):
+            oT_sb[n] = oT_pool.tile([P, RC, D], F32, name="oT_sb")
             for j in range(RC):
-                nc.scalar.activation(oT_sb[n][:, j, :], oT_ps[n][j // 2][:, j % 2, 0:D], COPY, scale=rinv[:, j, :])
+                nc.scalar.activation(oT_sb[n][:, j, :], oT_ps[n][j // 2][:, j % 2, 0:D], COPY, scale=rinv[n][:, j, :])
+
+        def transpose(n):
+            o_ps[n] = ps_t.tile([P, R], F32, name="o_ps")
+            for j in range(RC):
+                nc.tensor.transpose(o_ps[n][:, j * P : (j + 1) * P], oT_sb[n][:, j, :], ident_f[:])
 
         def store(n):
             h, b = blocks[n]
-            o_ps = ps_t.tile([P, R], F32, name="o_ps")
-            for j in range(RC):
-                nc.tensor.transpose(o_ps[:, j * P : (j + 1) * P], oT_sb[n][:, j, :], ident_f[:])
             o_sb = o_pool.tile([P, R], F32, name="o_sb")
-            nc.vector.tensor_copy(o_sb[:], o_ps[:])
+            nc.vector.tensor_copy(o_sb[:], o_ps[n][:])
             nc.sync.dma_start(out[h * D : (h + 1) * D, b * R : (b + 1) * R], o_sb[:])
 
         ident_f = held.tile([P, P], F32, name="ident_f")
@@ -129,8 +154,11 @@ def tile_streamingattentionsink_b_kernel(tc, kc, q, vals, rc, rs, offs, out):
         nc.sync.dma_start(rs_partner[0:HALF, :], rs[HALF:D, :])
         nc.sync.dma_start(rs_partner[HALF:D, :], rs[0:HALF, :])
         vals_heads = vals.rearrange("(n p) (h d) -> p h n d", p=P, h=H)
-        for h in range(H):
-            load_head(h)
+        load_queries(0)
+        load_head(0)
+        for n in range(1, B):
+            load_queries(n)
+        load_head(1)
 
         cos_q = rc_sb[:, T - 1 : T]
         sin_q = rs_partner[:, T - 1 : T]
@@ -140,23 +168,41 @@ def tile_streamingattentionsink_b_kernel(tc, kc, q, vals, rc, rs, offs, out):
         nc.vector.scalar_tensor_tensor(rotT[:, 0:HALF], ident_f[:, 0:HALF], cos_q, sin_diag[:, HALF:P], MULT, ADD)
         nc.vector.scalar_tensor_tensor(rotT[:, HALF:P], ident_f[:, HALF:P], cos_q, sin_diag[:, 0:HALF], MULT, ADD)
 
-        for n in range(3):
-            look_up_keys(n)
-        for n in range(2):
-            rotate_queries(n)
-            add_halves(n)
+        rotate_queries(0)
+        look_up_partners(0)
+        look_up_own(0)
+        look_up_partners(1)
+        look_up_partners(2)
+        add_terms(0)
+        round_queries(0)
+        rotate_queries(1)
+        look_up_partners(3)
+        for n in range(B, B + 2):
+            load_queries(n)
         for i in range(NB + 2):
-            if 0 <= i - 2:
-                divide(i - 2)
+            if i + 1 < NB:
+                look_up_own(i + 1)
+                round_queries(i + 1)
             if i < NB:
                 scores(i)
-            if i + 3 < NB:
-                look_up_keys(i + 3)
-            if i + 2 < NB:
-                rotate_queries(i + 2)
             if 0 <= i - 2:
-                store(i - 2)
-            if i + 2 < NB:
-                add_halves(i + 2)
+                transpose(i - 2)
             if 0 <= i - 1 < NB:
                 weigh_values(i - 1)
+            if i + 2 < NB:
+                rotate_queries(i + 2)
+            if i < NB:
+                exponentials(i)
+            if i + 1 < NB:
+                add_terms(i + 1)
+            if i + 4 < NB:
+                look_up_partners(i + 4)
+            if i + 6 < NB:
+                load_queries(i + 6)
+            if i % B == 0 and i // B + 2 < H:
+                load_head(i // B + 2)
+            if 0 <= i - 2:
+                store(i - 2)
+            if 0 <= i - 1 < NB:
+                invert_sums(i - 1)
+                divide(i - 1)

@@ -36,19 +36,15 @@ def tile_streamingattentionsink_b_kernel(tc, kc, q, vals, rc, rs, offs, out):
         vals_pool = ctx.enter_context(tc.tile_pool(name="vals_pool", bufs=2))
         qr_pool = ctx.enter_context(tc.tile_pool(name="qr_pool", bufs=4))
         own_pool = ctx.enter_context(tc.tile_pool(name="own_pool", bufs=3))
-        swap_pool = ctx.enter_context(tc.tile_pool(name="swap_pool", bufs=3))
         kr_pool = ctx.enter_context(tc.tile_pool(name="kr_pool", bufs=4))
         e_pool = ctx.enter_context(tc.tile_pool(name="e_pool", bufs=3))
         small = ctx.enter_context(tc.tile_pool(name="small", bufs=3))
         oT_pool = ctx.enter_context(tc.tile_pool(name="oT_pool", bufs=2))
         o_pool = ctx.enter_context(tc.tile_pool(name="o_pool", bufs=6))
-        ps_s = ctx.enter_context(tc.psum_pool(name="ps_s", bufs=4))
-        ps_o = ctx.enter_context(tc.psum_pool(name="ps_o", bufs=2))
-        ps_t = ctx.enter_context(tc.psum_pool(name="ps_t", bufs=1))
-        ps_q = ctx.enter_context(tc.psum_pool(name="ps_q", bufs=1))
+        psum = ctx.enter_context(tc.psum_pool(name="psum", bufs=8))
 
         blocks = [(h, b) for h in range(H) for b in range(B)]
-        keys, crossed, moved, own, kr, queries, q_ps, qr = {}, {}, {}, {}, {}, {}, {}, {}
+        keys, partner, own, kr, queries, q_ps, qr = {}, {}, {}, {}, {}, {}, {}
         vals_sb, s_ps, e, oT_ps, rinv, oT_sb, o_ps = {}, {}, {}, {}, {}, {}, {}
 
         def load_head(h):
@@ -65,7 +61,7 @@ def tile_streamingattentionsink_b_kernel(tc, kc, q, vals, rc, rs, offs, out):
             nc.sync.dma_start(queries[n][:], q[h * D : (h + 1) * D, b * R : (b + 1) * R])
 
         def rotate_queries(n):
-            q_ps[n] = ps_q.tile([P, R], F32, name="q_ps")
+            q_ps[n] = psum.tile([P, R], F32, name="q_ps", tag="bank")
             nc.tensor.matmul(q_ps[n][:], lhsT=rotT[:], rhs=queries[n][:], start=True, stop=True)
 
         def round_queries(n):
@@ -77,15 +73,10 @@ def tile_streamingattentionsink_b_kernel(tc, kc, q, vals, rc, rs, offs, out):
 
         def look_up_partners(n):
             h, b = blocks[n]
-            g, place = (n + 1) // 2, (n + 1) % 2
-            if n == 0 or place == 0:
-                crossed[g] = swap_pool.tile([P, 2, T], F32, name="crossed")
-                moved[g] = swap_pool.tile([P, 2, T], F32, name="moved")
-            nc.vector.tensor_tensor(crossed[g][:, place, :], keys[h][:].indirect(piece(b)), rs_partner[:], MULT)
-            if place == 1 or n == NB - 1:
-                used = slice(1, 2) if n == 0 else slice(0, place + 1)
-                nc.sync.dma_start(moved[g][0:HALF, used, :], crossed[g][HALF:P, used, :])
-                nc.gpsimd.dma_start(moved[g][HALF:P, used, :], crossed[g][0:HALF, used, :])
+            crossed = own_pool.tile([P, T], F32, name="crossed")
+            nc.vector.tensor_tensor(crossed[:], keys[h][:].indirect(piece(b)), rs_partner[:], MULT)
+            partner[n] = psum.tile([P, T], F32, name="partner", tag="bank")
+            nc.tensor.matmul(partner[n][:], lhsT=swap[:], rhs=crossed[:], start=True, stop=True)
 
         def look_up_own(n):
             h, b = blocks[n]
@@ -94,10 +85,10 @@ def tile_streamingattentionsink_b_kernel(tc, kc, q, vals, rc, rs, offs, out):
 
         def add_terms(n):
             kr[n] = kr_pool.tile([P, T], BF16, name="kr")
-            nc.vector.tensor_tensor(kr[n][:], own[n][:], moved[(n + 1) // 2][:, (n + 1) % 2, :], ADD)
+            nc.vector.tensor_tensor(kr[n][:], own[n][:], partner[n][:], ADD)
 
         def scores(n):
-            s_ps[n] = [ps_s.tile([P, R], F32, name="s_ps") for _ in range(TC)]
+            s_ps[n] = [psum.tile([P, R], F32, name="s_ps", tag="bank") for _ in range(TC)]
             for c in range(TC):
                 nc.tensor.matmul(s_ps[n][c][:], lhsT=kr[n][:, c * P : (c + 1) * P], rhs=qr[n][:], start=True, stop=True)
 
@@ -110,7 +101,7 @@ def tile_streamingattentionsink_b_kernel(tc, kc, q, vals, rc, rs, offs, out):
             h, b = blocks[n]
             oT_ps[n] = []
             for pair in range(RC // 2):
-                oT_ps[n].append(ps_o.tile([P, 2, BANK // 2], F32, name="oT_ps"))
+                oT_ps[n].append(psum.tile([P, 2, BANK // 2], F32, name="oT_ps", tag="bank"))
                 for jj in range(2):
                     j = 2 * pair + jj
                     for c in range(TC):
@@ -129,18 +120,19 @@ def tile_streamingattentionsink_b_kernel(tc, kc, q, vals, rc, rs, offs, out):
 
         def divide(n):
             oT_sb[n] = oT_pool.tile([P, RC, D], F32, name="oT_sb")
-            for j in range(RC):
-                nc.scalar.activation(oT_sb[n][:, j, :], oT_ps[n][j // 2][:, j % 2, 0:D], COPY, scale=rinv[n][:, j, :])
+            for pair in range(RC // 2):
+                js = slice(2 * pair, 2 * pair + 2)
+                nc.vector.tensor_tensor(oT_sb[n][:, js, :], oT_ps[n][pair][:, :, 0:D], rinv[n][:, js, :].to_broadcast([P, 2, D]), MULT)
 
         def transpose(n):
-            o_ps[n] = ps_t.tile([P, R], F32, name="o_ps")
+            o_ps[n] = psum.tile([P, R], F32, name="o_ps", tag="bank")
             for j in range(RC):
                 nc.tensor.transpose(o_ps[n][:, j * P : (j + 1) * P], oT_sb[n][:, j, :], ident_f[:])
 
         def store(n):
             h, b = blocks[n]
             o_sb = o_pool.tile([P, R], F32, name="o_sb")
-            nc.vector.tensor_copy(o_sb[:], o_ps[n][:])
+            nc.scalar.copy(o_sb[:], o_ps[n][:])
             nc.sync.dma_start(out[h * D : (h + 1) * D, b * R : (b + 1) * R], o_sb[:])
 
         ident_f = held.tile([P, P], F32, name="ident_f")
@@ -154,9 +146,8 @@ def tile_streamingattentionsink_b_kernel(tc, kc, q, vals, rc, rs, offs, out):
         nc.sync.dma_start(rs_partner[0:HALF, :], rs[HALF:D, :])
         nc.sync.dma_start(rs_partner[HALF:D, :], rs[0:HALF, :])
         vals_heads = vals.rearrange("(n p) (h d) -> p h n d", p=P, h=H)
-        load_queries(0)
         load_head(0)
-        for n in range(1, B):
+        for n in range(B):
             load_queries(n)
         load_head(1)
 
@@ -168,15 +159,17 @@ def tile_streamingattentionsink_b_kernel(tc, kc, q, vals, rc, rs, offs, out):
         nc.vector.scalar_tensor_tensor(rotT[:, 0:HALF], ident_f[:, 0:HALF], cos_q, sin_diag[:, HALF:P], MULT, ADD)
         nc.vector.scalar_tensor_tensor(rotT[:, HALF:P], ident_f[:, HALF:P], cos_q, sin_diag[:, 0:HALF], MULT, ADD)
 
+        swap = held.tile([P, P], F32, name="swap")
+        nc.gpsimd.tensor_copy(swap[:, 0:HALF], ident_f[:, HALF:P])
+        nc.gpsimd.tensor_copy(swap[:, HALF:P], ident_f[:, 0:HALF])
+
         rotate_queries(0)
         look_up_partners(0)
         look_up_own(0)
         look_up_partners(1)
-        look_up_partners(2)
         add_terms(0)
         round_queries(0)
         rotate_queries(1)
-        look_up_partners(3)
         for n in range(B, B + 2):
             load_queries(n)
         for i in range(NB + 2):
@@ -195,8 +188,8 @@ def tile_streamingattentionsink_b_kernel(tc, kc, q, vals, rc, rs, offs, out):
                 exponentials(i)
             if i + 1 < NB:
                 add_terms(i + 1)
-            if i + 4 < NB:
-                look_up_partners(i + 4)
+            if i + 2 < NB:
+                look_up_partners(i + 2)
             if i + 6 < NB:
                 load_queries(i + 6)
             if i % B == 0 and i // B + 2 < H:

@@ -34,6 +34,8 @@ def tile_streamingattentionsink_b_kernel(tc, kc, q, vals, rc, rs, offs, out):
         key_pool = ctx.enter_context(tc.tile_pool(name="key_pool", bufs=2))
         q_pool = ctx.enter_context(tc.tile_pool(name="q_pool", bufs=B))
         vals_pool = ctx.enter_context(tc.tile_pool(name="vals_pool", bufs=2))
+        qp_pool = ctx.enter_context(tc.tile_pool(name="qp_pool", bufs=2))
+        qs_pool = ctx.enter_context(tc.tile_pool(name="qs_pool", bufs=2))
         qr_pool = ctx.enter_context(tc.tile_pool(name="qr_pool", bufs=4))
         own_pool = ctx.enter_context(tc.tile_pool(name="own_pool", bufs=3))
         kr_pool = ctx.enter_context(tc.tile_pool(name="kr_pool", bufs=4))
@@ -44,7 +46,7 @@ def tile_streamingattentionsink_b_kernel(tc, kc, q, vals, rc, rs, offs, out):
         psum = ctx.enter_context(tc.psum_pool(name="psum", bufs=8))
 
         blocks = [(h, b) for h in range(H) for b in range(B)]
-        keys, partner, own, kr, queries, q_ps, qr = {}, {}, {}, {}, {}, {}, {}
+        keys, partner, own, kr, partners, q_sin, queries, q_ps, qr = {}, {}, {}, {}, {}, {}, {}, {}, {}
         vals_sb, s_ps, e, oT_ps, rinv, oT_sb, o_ps = {}, {}, {}, {}, {}, {}, {}
 
         def load_head(h):
@@ -55,17 +57,32 @@ def tile_streamingattentionsink_b_kernel(tc, kc, q, vals, rc, rs, offs, out):
             nc.gpsimd.memset(vals_sb[h][:, :, D:VW], 1.0)
             nc.sync.dma_start(vals_sb[h][:, :, 0:D], vals_heads[:, h, :, :])
 
+        def by_elements(n):
+            return n % 2 == 1 and n > 2
+
         def load_queries(n):
             h, b = blocks[n]
+            columns = slice(b * R, (b + 1) * R)
             queries[n] = q_pool.tile([P, R], F32, name="queries")
-            nc.sync.dma_start(queries[n][:], q[h * D : (h + 1) * D, b * R : (b + 1) * R])
+            nc.sync.dma_start(queries[n][:], q[h * D : (h + 1) * D, columns])
+            if by_elements(n):
+                partners[n] = qp_pool.tile([P, R], F32, name="partners")
+                nc.sync.dma_start(partners[n][0:HALF, :], q[h * D + HALF : (h + 1) * D, columns])
+                nc.gpsimd.dma_start(partners[n][HALF:D, :], q[h * D : h * D + HALF, columns])
 
         def rotate_queries(n):
+            if by_elements(n):
+                q_sin[n] = qs_pool.tile([P, R], F32, name="q_sin")
+                nc.scalar.activation(q_sin[n][:], partners[n][:], COPY, scale=sin_own)
+                return
             q_ps[n] = psum.tile([P, R], F32, name="q_ps", tag="bank")
             nc.tensor.matmul(q_ps[n][:], lhsT=rotT[:], rhs=queries[n][:], start=True, stop=True)
 
         def round_queries(n):
             qr[n] = qr_pool.tile([P, R], BF16, name="qr")
+            if by_elements(n):
+                nc.vector.scalar_tensor_tensor(qr[n][:], queries[n][:], cos_q, q_sin[n][:], MULT, ADD)
+                return
             nc.scalar.copy(qr[n][:], q_ps[n][:])
 
         def piece(b):
@@ -145,6 +162,9 @@ def tile_streamingattentionsink_b_kernel(tc, kc, q, vals, rc, rs, offs, out):
         rs_partner = held.tile([P, T], F32, name="rs_partner")
         nc.sync.dma_start(rs_partner[0:HALF, :], rs[HALF:D, :])
         nc.sync.dma_start(rs_partner[HALF:D, :], rs[0:HALF, :])
+        sin_sb = held.tile([P, 64], F32, name="sin_sb")
+        nc.sync.dma_start(sin_sb[:], rs[:, T - 64 : T])
+        sin_own = sin_sb[:, 63:64]
         vals_heads = vals.rearrange("(n p) (h d) -> p h n d", p=P, h=H)
         load_head(0)
         for n in range(B):

@@ -23,6 +23,7 @@ NB = H * B
 SCALE = 1.0 / math.sqrt(D)
 VW = D + 16
 PIECE = 512
+LAST = 64
 BANK = 512
 FLOPS = 4 * H * B * T * R * D
 
@@ -33,11 +34,11 @@ def tile_streamingattentionsink_b_kernel(tc, kc, q, vals, rc, rs, offs, out):
         held = ctx.enter_context(tc.tile_pool(name="held", bufs=1))
         key_pool = ctx.enter_context(tc.tile_pool(name="key_pool", bufs=2))
         q_pool = ctx.enter_context(tc.tile_pool(name="q_pool", bufs=B))
-        vals_pool = ctx.enter_context(tc.tile_pool(name="vals_pool", bufs=2))
-        qp_pool = ctx.enter_context(tc.tile_pool(name="qp_pool", bufs=2))
+        vals_pool = ctx.enter_context(tc.tile_pool(name="vals_pool", bufs=H))
         qs_pool = ctx.enter_context(tc.tile_pool(name="qs_pool", bufs=2))
         qr_pool = ctx.enter_context(tc.tile_pool(name="qr_pool", bufs=4))
-        own_pool = ctx.enter_context(tc.tile_pool(name="own_pool", bufs=3))
+        own_pool = ctx.enter_context(tc.tile_pool(name="own_pool", bufs=1))
+        crossed_pool = ctx.enter_context(tc.tile_pool(name="crossed_pool", bufs=2))
         kr_pool = ctx.enter_context(tc.tile_pool(name="kr_pool", bufs=4))
         e_pool = ctx.enter_context(tc.tile_pool(name="e_pool", bufs=3))
         small = ctx.enter_context(tc.tile_pool(name="small", bufs=3))
@@ -46,34 +47,41 @@ def tile_streamingattentionsink_b_kernel(tc, kc, q, vals, rc, rs, offs, out):
         psum = ctx.enter_context(tc.psum_pool(name="psum", bufs=8))
 
         blocks = [(h, b) for h in range(H) for b in range(B)]
-        keys, partner, own, kr, partners, q_sin, queries, q_ps, qr = {}, {}, {}, {}, {}, {}, {}, {}, {}
+        keys, partner, own, kr, shifted, q_sin, queries, q_ps, qr = {}, {}, {}, {}, {}, {}, {}, {}, {}
         vals_sb, s_ps, e, oT_ps, rinv, oT_sb, o_ps = {}, {}, {}, {}, {}, {}, {}
 
-        def load_head(h):
+        def load_keys(h):
             keys[h] = key_pool.tile([P, S], F32, name="keys")
             for s in range(0, S, PIECE):
                 nc.sync.dma_start(keys[h][:, s : s + PIECE], kc[h * D : (h + 1) * D, s : s + PIECE])
+
+        def load_vals(h):
             vals_sb[h] = vals_pool.tile([P, N // P, VW], BF16, name="vals_sb")
             nc.gpsimd.memset(vals_sb[h][:, :, D:VW], 1.0)
             nc.sync.dma_start(vals_sb[h][:, :, 0:D], vals_heads[:, h, :, :])
 
         def by_elements(n):
-            return n % 2 == 1 and n > 2
+            return n % 2 == 1 and n >= B
+
+        def load_shifted(h):
+            first = h * D + HALF
+            last = min(first + D, H * D)
+            shifted[h] = held.tile([P, B // 2, R], F32, name="shifted%d" % h)
+            odd = q[first:last, :].rearrange("p (k t r) -> p k t r", k=B // 2, t=2)[:, :, 1, :]
+            nc.sync.dma_start(shifted[h][0 : last - first, :, :], odd)
 
         def load_queries(n):
             h, b = blocks[n]
             columns = slice(b * R, (b + 1) * R)
             queries[n] = q_pool.tile([P, R], F32, name="queries")
             nc.sync.dma_start(queries[n][:], q[h * D : (h + 1) * D, columns])
-            if by_elements(n):
-                partners[n] = qp_pool.tile([P, R], F32, name="partners")
-                nc.sync.dma_start(partners[n][0:HALF, :], q[h * D + HALF : (h + 1) * D, columns])
-                nc.gpsimd.dma_start(partners[n][HALF:D, :], q[h * D : h * D + HALF, columns])
 
         def rotate_queries(n):
             if by_elements(n):
+                h, b = blocks[n]
                 q_sin[n] = qs_pool.tile([P, R], F32, name="q_sin")
-                nc.scalar.activation(q_sin[n][:], partners[n][:], COPY, scale=sin_own)
+                for half, rows in ((slice(0, HALF), shifted[h]), (slice(HALF, P), shifted[h - 1])):
+                    nc.scalar.activation(q_sin[n][half, :], rows[half, b // 2, :], COPY, scale=sin_own[half, :])
                 return
             q_ps[n] = psum.tile([P, R], F32, name="q_ps", tag="bank")
             nc.tensor.matmul(q_ps[n][:], lhsT=rotT[:], rhs=queries[n][:], start=True, stop=True)
@@ -90,7 +98,7 @@ def tile_streamingattentionsink_b_kernel(tc, kc, q, vals, rc, rs, offs, out):
 
         def look_up_partners(n):
             h, b = blocks[n]
-            crossed = own_pool.tile([P, T], F32, name="crossed")
+            crossed = crossed_pool.tile([P, T], F32, name="crossed")
             nc.vector.tensor_tensor(crossed[:], keys[h][:].indirect(piece(b)), rs_partner[:], MULT)
             partner[n] = psum.tile([P, T], F32, name="partner", tag="bank")
             nc.tensor.matmul(partner[n][:], lhsT=swap[:], rhs=crossed[:], start=True, stop=True)
@@ -137,9 +145,8 @@ def tile_streamingattentionsink_b_kernel(tc, kc, q, vals, rc, rs, offs, out):
 
         def divide(n):
             oT_sb[n] = oT_pool.tile([P, RC, D], F32, name="oT_sb")
-            for pair in range(RC // 2):
-                js = slice(2 * pair, 2 * pair + 2)
-                nc.vector.tensor_tensor(oT_sb[n][:, js, :], oT_ps[n][pair][:, :, 0:D], rinv[n][:, js, :].to_broadcast([P, 2, D]), MULT)
+            for j in range(RC):
+                nc.scalar.activation(oT_sb[n][:, j, :], oT_ps[n][j // 2][:, j % 2, 0:D], COPY, scale=rinv[n][:, j, :])
 
         def transpose(n):
             o_ps[n] = psum.tile([P, R], F32, name="o_ps", tag="bank")
@@ -149,7 +156,7 @@ def tile_streamingattentionsink_b_kernel(tc, kc, q, vals, rc, rs, offs, out):
         def store(n):
             h, b = blocks[n]
             o_sb = o_pool.tile([P, R], F32, name="o_sb")
-            nc.scalar.copy(o_sb[:], o_ps[n][:])
+            nc.vector.tensor_copy(o_sb[:], o_ps[n][:])
             nc.sync.dma_start(out[h * D : (h + 1) * D, b * R : (b + 1) * R], o_sb[:])
 
         ident_f = held.tile([P, P], F32, name="ident_f")
@@ -157,21 +164,29 @@ def tile_streamingattentionsink_b_kernel(tc, kc, q, vals, rc, rs, offs, out):
 
         offsets = held.tile([P, N // 16], U16, name="offsets")
         nc.sync.dma_start(offsets[:], offs)
-        rc_sb = held.tile([P, T], F32, name="rc_sb")
-        nc.sync.dma_start(rc_sb[:], rc)
         rs_partner = held.tile([P, T], F32, name="rs_partner")
         nc.sync.dma_start(rs_partner[0:HALF, :], rs[HALF:D, :])
         nc.sync.dma_start(rs_partner[HALF:D, :], rs[0:HALF, :])
-        sin_sb = held.tile([P, 64], F32, name="sin_sb")
-        nc.sync.dma_start(sin_sb[:], rs[:, T - 64 : T])
-        sin_own = sin_sb[:, 63:64]
+        cos_last = held.tile([P, LAST], F32, name="cos_last")
+        nc.sync.dma_start(cos_last[:], rc[:, T - LAST : T])
+        load_queries(0)
+        load_keys(0)
+        rc_sb = held.tile([P, T], F32, name="rc_sb")
+        nc.sync.dma_start(rc_sb[:], rc)
+        load_queries(1)
         vals_heads = vals.rearrange("(n p) (h d) -> p h n d", p=P, h=H)
-        load_head(0)
-        for n in range(B):
-            load_queries(n)
-        load_head(1)
+        load_vals(0)
+        load_queries(2)
+        load_queries(3)
+        load_keys(1)
+        load_vals(1)
+        sin_last = held.tile([P, LAST], F32, name="sin_last")
+        nc.sync.dma_start(sin_last[:], rs[:, T - LAST : T])
+        sin_own = sin_last[:, LAST - 1 : LAST]
+        for h in range(H):
+            load_shifted(h)
 
-        cos_q = rc_sb[:, T - 1 : T]
+        cos_q = cos_last[:, LAST - 1 : LAST]
         sin_q = rs_partner[:, T - 1 : T]
         sin_diag = held.tile([P, P], F32, name="sin_diag")
         nc.vector.tensor_scalar_mul(sin_diag[:], ident_f[:], sin_q)
@@ -189,17 +204,17 @@ def tile_streamingattentionsink_b_kernel(tc, kc, q, vals, rc, rs, offs, out):
         look_up_partners(1)
         add_terms(0)
         round_queries(0)
-        rotate_queries(1)
         for n in range(B, B + 2):
             load_queries(n)
         for i in range(NB + 2):
             if i + 1 < NB:
                 look_up_own(i + 1)
-                round_queries(i + 1)
             if i < NB:
                 scores(i)
-            if 0 <= i - 2:
-                transpose(i - 2)
+            if i == 0:
+                rotate_queries(1)
+            if i + 1 < NB:
+                round_queries(i + 1)
             if 0 <= i - 1 < NB:
                 weigh_values(i - 1)
             if i + 2 < NB:
@@ -213,9 +228,11 @@ def tile_streamingattentionsink_b_kernel(tc, kc, q, vals, rc, rs, offs, out):
             if i + 6 < NB:
                 load_queries(i + 6)
             if i % B == 0 and i // B + 2 < H:
-                load_head(i // B + 2)
-            if 0 <= i - 2:
-                store(i - 2)
+                load_keys(i // B + 2)
+                load_vals(i // B + 2)
             if 0 <= i - 1 < NB:
                 invert_sums(i - 1)
                 divide(i - 1)
+            if 0 <= i - 2:
+                transpose(i - 2)
+                store(i - 2)

@@ -50,10 +50,13 @@ def tile_streamingattentionsink_b_kernel(tc, kc, q, vals, rc, rs, offs, out):
         keys, partner, own, kr, shifted, q_sin, queries, q_ps, qr = {}, {}, {}, {}, {}, {}, {}, {}, {}
         vals_sb, s_ps, e, oT_ps, rinv, oT_sb, o_ps = {}, {}, {}, {}, {}, {}, {}
 
+        def load_key_columns(h, first, last):
+            for s in range(first, last, PIECE):
+                nc.sync.dma_start(keys[h][:, s : s + PIECE], kc[h * D : (h + 1) * D, s : s + PIECE])
+
         def load_keys(h):
             keys[h] = key_pool.tile([P, S], F32, name="keys")
-            for s in range(0, S, PIECE):
-                nc.sync.dma_start(keys[h][:, s : s + PIECE], kc[h * D : (h + 1) * D, s : s + PIECE])
+            load_key_columns(h, 0, S)
 
         def load_vals(h):
             vals_sb[h] = vals_pool.tile([P, N // P, VW], BF16, name="vals_sb")
@@ -155,9 +158,11 @@ def tile_streamingattentionsink_b_kernel(tc, kc, q, vals, rc, rs, offs, out):
 
         def store(n):
             h, b = blocks[n]
-            o_sb = o_pool.tile([P, R], F32, name="o_sb")
-            nc.vector.tensor_copy(o_sb[:], o_ps[n][:])
-            nc.sync.dma_start(out[h * D : (h + 1) * D, b * R : (b + 1) * R], o_sb[:])
+            width = R // 2 if n == NB - 1 else R
+            for r in range(0, R, width):
+                o_sb = o_pool.tile([P, width], F32, name="o_sb")
+                nc.vector.tensor_copy(o_sb[:], o_ps[n][:, r : r + width])
+                nc.sync.dma_start(out[h * D : (h + 1) * D, b * R + r : b * R + r + width], o_sb[:])
 
         ident_f = held.tile([P, P], F32, name="ident_f")
         make_identity(nc, ident_f[:])
@@ -169,8 +174,10 @@ def tile_streamingattentionsink_b_kernel(tc, kc, q, vals, rc, rs, offs, out):
         nc.sync.dma_start(rs_partner[HALF:D, :], rs[0:HALF, :])
         cos_last = held.tile([P, LAST], F32, name="cos_last")
         nc.sync.dma_start(cos_last[:], rc[:, T - LAST : T])
+        keys[0] = key_pool.tile([P, S], F32, name="keys")
+        load_key_columns(0, 0, S // 2)
         load_queries(0)
-        load_keys(0)
+        load_key_columns(0, S // 2, S)
         rc_sb = held.tile([P, T], F32, name="rc_sb")
         nc.sync.dma_start(rc_sb[:], rc)
         load_queries(1)

import math
from contextlib import ExitStack

import concourse.mybir as mybir
from concourse.masks import make_identity

F32 = mybir.dt.float32
BF16 = mybir.dt.bfloat16
U16 = mybir.dt.uint16
MULT = mybir.AluOpType.mult
ADD = mybir.AluOpType.add
EXP = mybir.ActivationFunctionType.Exp
COPY = mybir.ActivationFunctionType.Copy

P = 128
H, D, HALF = 4, 128, 64
B, T, R = 4, 512, 512
S = 4096
N = B * T
TC = T // P
RC = R // P
NB = H * B
SCALE = 1.0 / math.sqrt(D)
VW = D + 16
PIECE = 512
LAST = 64
BANK = 512
FLOPS = 4 * H * B * T * R * D


def tile_streamingattentionsink_b_kernel(tc, kc, q, vals, rc, rs, offs, out):
    nc = tc.nc
    with ExitStack() as ctx:
        held = ctx.enter_context(tc.tile_pool(name="held", bufs=1))
        key_pool = ctx.enter_context(tc.tile_pool(name="key_pool", bufs=2))
        q_pool = ctx.enter_context(tc.tile_pool(name="q_pool", bufs=B))
        vals_pool = ctx.enter_context(tc.tile_pool(name="vals_pool", bufs=H))
        qs_pool = ctx.enter_context(tc.tile_pool(name="qs_pool", bufs=2))
        qr_pool = ctx.enter_context(tc.tile_pool(name="qr_pool", bufs=4))
        own_pool = ctx.enter_context(tc.tile_pool(name="own_pool", bufs=1))
        crossed_pool = ctx.enter_context(tc.tile_pool(name="crossed_pool", bufs=2))
        kr_pool = ctx.enter_context(tc.tile_pool(name="kr_pool", bufs=4))
        e_pool = ctx.enter_context(tc.tile_pool(name="e_pool", bufs=3))
        small = ctx.enter_context(tc.tile_pool(name="small", bufs=3))
        oT_pool = ctx.enter_context(tc.tile_pool(name="oT_pool", bufs=2))
        o_pool = ctx.enter_context(tc.tile_pool(name="o_pool", bufs=6))
        psum = ctx.enter_context(tc.psum_pool(name="psum", bufs=8))

        blocks = [(h, b) for h in range(H) for b in range(B)]
        keys, partner, own, kr, shifted, q_sin, queries, q_ps, qr = {}, {}, {}, {}, {}, {}, {}, {}, {}
        vals_sb, s_ps, e, oT_ps, rinv, oT_sb, o_ps = {}, {}, {}, {}, {}, {}, {}

        def load_key_columns(h, first, last):
            for s in range(first, last, PIECE):
                nc.sync.dma_start(keys[h][:, s : s + PIECE], kc[h * D : (h + 1) * D, s : s + PIECE])

        def load_keys(h):
            keys[h] = key_pool.tile([P, S], F32, name="keys")
            load_key_columns(h, 0, S)

        def load_vals(h):
            vals_sb[h] = vals_pool.tile([P, N // P, VW], BF16, name="vals_sb")
            nc.gpsimd.memset(vals_sb[h][:, :, D:VW], 1.0)
            nc.sync.dma_start(vals_sb[h][:, :, 0:D], vals_heads[:, h, :, :])

        def by_elements(n):
            return n % 2 == 1 and n >= B

        def load_shifted(h):
            first = h * D + HALF
            last = min(first + D, H * D)
            shifted[h] = held.tile([P, B // 2, R], F32, name="shifted%d" % h)
            odd = q[first:last, :].rearrange("p (k t r) -> p k t r", k=B // 2, t=2)[:, :, 1, :]
            nc.sync.dma_start(shifted[h][0 : last - first, :, :], odd)

        def load_queries(n):
            h, b = blocks[n]
            columns = slice(b * R, (b + 1) * R)
            queries[n] = q_pool.tile([P, R], F32, name="queries")
            nc.sync.dma_start(queries[n][:], q[h * D : (h + 1) * D, columns])

        def rotate_queries(n):
            if by_elements(n):
                h, b = blocks[n]
                q_sin[n] = qs_pool.tile([P, R], F32, name="q_sin")
                for half, rows in ((slice(0, HALF), shifted[h]), (slice(HALF, P), shifted[h - 1])):
                    nc.scalar.activation(q_sin[n][half, :], rows[half, b // 2, :], COPY, scale=sin_own[half, :])
                return
            q_ps[n] = psum.tile([P, R], F32, name="q_ps", tag="bank")
            nc.tensor.matmul(q_ps[n][:], lhsT=rotT[:], rhs=queries[n][:], start=True, stop=True)

        def round_queries(n):
            qr[n] = qr_pool.tile([P, R], BF16, name="qr")
            if by_elements(n):
                nc.vector.scalar_tensor_tensor(qr[n][:], queries[n][:], cos_q, q_sin[n][:], MULT, ADD)
                return
            nc.scalar.copy(qr[n][:], q_ps[n][:])

        def piece(b):
            return offsets[:, b * (T // 16) : (b + 1) * (T // 16)]

        def look_up_partners(n):
            h, b = blocks[n]
            crossed = crossed_pool.tile([P, T], F32, name="crossed")
            nc.vector.tensor_tensor(crossed[:], keys[h][:].indirect(piece(b)), rs_partner[:], MULT)
            partner[n] = psum.tile([P, T], F32, name="partner", tag="bank")
            nc.tensor.matmul(partner[n][:], lhsT=swap[:], rhs=crossed[:], start=True, stop=True)

        def look_up_own(n):
            h, b = blocks[n]
            own[n] = own_pool.tile([P, T], F32, name="own")
            nc.vector.tensor_tensor(own[n][:], keys[h][:].indirect(piece(b)), rc_sb[:], MULT)

        def add_terms(n):
            kr[n] = kr_pool.tile([P, T], BF16, name="kr")
            nc.vector.tensor_tensor(kr[n][:], own[n][:], partner[n][:], ADD)

        def scores(n):
            s_ps[n] = [psum.tile([P, R], F32, name="s_ps", tag="bank") for _ in range(TC)]
            for c in range(TC):
                nc.tensor.matmul(s_ps[n][c][:], lhsT=kr[n][:, c * P : (c + 1) * P], rhs=qr[n][:], start=True, stop=True)

        def exponentials(n):
            e[n] = e_pool.tile([P, TC, R], BF16, name="e")
            for c in range(TC):
                nc.scalar.activation(e[n][:, c, :], s_ps[n][c][:], EXP, scale=SCALE)

        def weigh_values(n):
            h, b = blocks[n]
            oT_ps[n] = []
            for pair in range(RC // 2):
                oT_ps[n].append(psum.tile([P, 2, BANK // 2], F32, name="oT_ps", tag="bank"))
                for jj in range(2):
                    j = 2 * pair + jj
                    for c in range(TC):
                        nc.tensor.matmul(
                            oT_ps[n][pair][:, jj, 0 : D + 1],
                            lhsT=e[n][:, c, j * P : (j + 1) * P],
                            rhs=vals_sb[h][:, b * TC + c, 0 : D + 1],
                            start=(c == 0),
                            stop=(c == TC - 1),
                        )

        def invert_sums(n):
            rinv[n] = small.tile([P, RC, 1], F32, name="rinv")
            for pair in range(RC // 2):
                nc.vector.reciprocal(rinv[n][:, 2 * pair : 2 * pair + 2, :], oT_ps[n][pair][:, :, D : D + 1])

        def divide(n):
            oT_sb[n] = oT_pool.tile([P, RC, D], F32, name="oT_sb")
            for j in range(RC):
                nc.scalar.activation(oT_sb[n][:, j, :], oT_ps[n][j // 2][:, j % 2, 0:D], COPY, scale=rinv[n][:, j, :])

        def transpose(n):
            o_ps[n] = psum.tile([P, R], F32, name="o_ps", tag="bank")
            for j in range(RC):
                nc.tensor.transpose(o_ps[n][:, j * P : (j + 1) * P], oT_sb[n][:, j, :], ident_f[:])

        def store(n):
            h, b = blocks[n]
            width = R // 2 if n == NB - 1 else R
            for r in range(0, R, width):
                o_sb = o_pool.tile([P, width], F32, name="o_sb")
                nc.vector.tensor_copy(o_sb[:], o_ps[n][:, r : r + width])
                nc.sync.dma_start(out[h * D : (h + 1) * D, b * R + r : b * R + r + width], o_sb[:])

        ident_f = held.tile([P, P], F32, name="ident_f")
        make_identity(nc, ident_f[:])

        offsets = held.tile([P, N // 16], U16, name="offsets")
        nc.sync.dma_start(offsets[:], offs)
        rs_partner = held.tile([P, T], F32, name="rs_partner")
        nc.sync.dma_start(rs_partner[0:HALF, :], rs[HALF:D, :])
        nc.sync.dma_start(rs_partner[HALF:D, :], rs[0:HALF, :])
        cos_last = held.tile([P, LAST], F32, name="cos_last")
        nc.sync.dma_start(cos_last[:], rc[:, T - LAST : T])
        keys[0] = key_pool.tile([P, S], F32, name="keys")
        load_key_columns(0, 0, S // 2)
        load_queries(0)
        load_key_columns(0, S // 2, S)
        rc_sb = held.tile([P, T], F32, name="rc_sb")
        nc.sync.dma_start(rc_sb[:], rc)
        load_queries(1)
        vals_heads = vals.rearrange("(n p) (h d) -> p h n d", p=P, h=H)
        load_vals(0)
        load_queries(2)
        load_queries(3)
        load_keys(1)
        load_vals(1)
        sin_last = held.tile([P, LAST], F32, name="sin_last")
        nc.sync.dma_start(sin_last[:], rs[:, T - LAST : T])
        sin_own = sin_last[:, LAST - 1 : LAST]
        for h in range(H):
            load_shifted(h)

        cos_q = cos_last[:, LAST - 1 : LAST]
        sin_q = rs_partner[:, T - 1 : T]
        sin_diag = held.tile([P, P], F32, name="sin_diag")
        nc.vector.tensor_scalar_mul(sin_diag[:], ident_f[:], sin_q)
        rotT = held.tile([P, P], F32, name="rotT")
        nc.vector.scalar_tensor_tensor(rotT[:, 0:HALF], ident_f[:, 0:HALF], cos_q, sin_diag[:, HALF:P], MULT, ADD)
        nc.vector.scalar_tensor_tensor(rotT[:, HALF:P], ident_f[:, HALF:P], cos_q, sin_diag[:, 0:HALF], MULT, ADD)

        swap = held.tile([P, P], F32, name="swap")
        nc.gpsimd.tensor_copy(swap[:, 0:HALF], ident_f[:, HALF:P])
        nc.gpsimd.tensor_copy(swap[:, HALF:P], ident_f[:, 0:HALF])

        rotate_queries(0)
        look_up_partners(0)
        look_up_own(0)
        look_up_partners(1)
        add_terms(0)
        round_queries(0)
        for n in range(B, B + 2):
            load_queries(n)
        for i in range(NB + 2):
            if i + 1 < NB:
                look_up_own(i + 1)
            if i < NB:
                scores(i)
            if i == 0:
                rotate_queries(1)
            if i + 1 < NB:
                round_queries(i + 1)
            if 0 <= i - 1 < NB:
                weigh_values(i - 1)
            if i + 2 < NB:
                rotate_queries(i + 2)
            if i < NB:
                exponentials(i)
            if i + 1 < NB:
                add_terms(i + 1)
            if i + 2 < NB:
                look_up_partners(i + 2)
            if i + 6 < NB:
                load_queries(i + 6)
            if i % B == 0 and i // B + 2 < H:
                load_keys(i // B + 2)
                load_vals(i // B + 2)
            if 0 <= i - 1 < NB:
                invert_sums(i - 1)
                divide(i - 1)
            if 0 <= i - 2:
                transpose(i - 2)
                store(i - 2)
